import numpy as np
import ml_dtypes


def mxq(x, axis, fmt="e4m3"):
    dtype, down = {"e4m3": (ml_dtypes.float8_e4m3fn, 7), "e5m2": (ml_dtypes.float8_e5m2, 14)}[fmt]
    v = np.moveaxis(np.asarray(x, np.float32).astype(ml_dtypes.bfloat16).astype(np.float64), axis, -1)
    blocks = v.reshape(v.shape[:-1] + (-1, 32))
    amax = np.abs(blocks).max(-1, keepdims=True)
    byte = np.maximum(np.where(amax > 0, np.frexp(amax)[1] - 1 + 127, 0) - down, 1)
    scale = np.exp2(byte - 127.0)
    codes = (blocks / scale).astype(np.float32).astype(dtype).astype(np.float64)
    return np.moveaxis((codes * scale).reshape(v.shape), -1, axis)


WIDE = False


def mx_kscale(k):
    if not WIDE:
        return np.ones(k)
    levels = np.array([10, -10, 5, -5, 0])
    a = np.random.permutation(np.resize(levels, k // 512 * 4)).reshape(k // 512, 4)
    idx = np.arange(k)
    return np.exp2(a[idx // 512, idx % 128 // 32])


BF16 = ml_dtypes.bfloat16


def bf(x):
    return np.asarray(x, np.float32).astype(BF16)


def f64(x):
    return np.asarray(x).astype(np.float64)


S, T, H, D, QB = 4096, 1024, 4, 128, 512
E = H * D


def setup_inputs():
    t = mx_kscale(E)
    u = np.sign(np.random.standard_normal((H, D)))
    be = np.random.uniform(-1.2, 1.2, (S, H, 1))
    al = np.random.uniform(-1.7, 1.7, (T, H, 1))
    ramp = np.linspace(-1.0, 1.0, T)[:, None, None]
    return {"q": bf(np.random.standard_normal((S, H, D)) * 0.7 + be * u / D ** 0.25),
            "k": bf(np.random.standard_normal((T, H, D)) * 0.7 + al * u / D ** 0.25),
            "v": bf((1.5 + 0.5 * al * u + 0.4 * ramp + 0.25 * np.random.standard_normal((T, H, D))) * t.reshape(H, D)),
            "W_proj": bf(np.random.standard_normal((E, E)) / np.sqrt(E) / t[None, :])}


def reference(q, k, v, W_proj):
    q, k, v = f64(q), f64(k), f64(v)
    s, h, d = q.shape
    t = k.shape[0]
    causal_bias = (np.arange(s)[:, None] < np.arange(t)[None, :]).astype(np.float64) * -10000.0
    scale = 1.0 / np.sqrt(d)
    scores = q.transpose(1, 0, 2) @ k.transpose(1, 2, 0) * scale + causal_bias
    e = np.exp(scores - scores.max(-1, keepdims=True))
    vq = mxq(v.transpose(1, 0, 2), 1, "e4m3")
    av = np.concatenate([(mxq(e[:, i:i + QB, :min(i + QB, t)], 2, "e4m3") @ vq[:, :min(i + QB, t)]) for i in range(0, s, QB)], axis=1)
    out = (av / e.sum(-1, keepdims=True)).transpose(1, 0, 2).reshape(s, h * d)
    return mxq(out, 1, "e4m3") @ mxq(f64(W_proj), 1, "e4m3").T

@@ -1,0 +1,299 @@
+import math
+from contextlib import ExitStack
+
+import concourse.mybir as mybir
+from concourse.masks import make_identity
+
+S, T, H, D = 4096, 1024, 4, 128
+E = H * D
+FLOPS = 2 * S * T * D * H + 2 * (512 * 512 + 3584 * 1024) * D * H + 2 * S * E * E
+
+MANUAL = False
+
+BF16 = mybir.dt.bfloat16
+F32 = mybir.dt.float32
+U32 = mybir.dt.uint32
+U8 = mybir.dt.uint8
+FP8X4 = mybir.dt.float8_e4m3fn_x4
+ALU = mybir.AluOpType
+ACTF = mybir.ActivationFunctionType
+AX = mybir.AxisListType
+
+P = 128
+SCALE = 1.0 / math.sqrt(D)
+MASK_FILL = -131072.0
+GROUP_ORDER = list(range(8, 32)) + list(range(4, 8)) + list(range(0, 4))
+
+
+def tile_mha_t_kernel(tc, q, k, v, W_proj, out):
+    nc = tc.nc
+    with ExitStack() as ctx:
+        const = ctx.enter_context(tc.tile_pool(name="const", bufs=1))
+        work = ctx.enter_context(tc.tile_pool(name="work", bufs=3))
+        small = ctx.enter_context(tc.tile_pool(name="small", bufs=4))
+        ps_s = ctx.enter_context(tc.psum_pool(name="ps_s", bufs=4))
+        ps_t = ctx.enter_context(tc.psum_pool(name="ps_t", bufs=2))
+        ps_o = ctx.enter_context(tc.psum_pool(name="ps_o", bufs=1))
+        ps_m = ctx.enter_context(tc.psum_pool(name="ps_m", bufs=1))
+
+        k_sb = const.tile([P, 2, 4, E], BF16, name="k_sb")
+        v_sb = const.tile([P, 2, 4, E], BF16, name="v_sb")
+        w_sb = const.tile([P, 4, E], BF16, name="w_sb")
+        q_sb = const.tile([P, 32, E], BF16, name="q_sb")
+        q_view = q.rearrange("(i p) h d -> p i (h d)", p=P)
+        nc.sync.dma_start(out=k_sb[:], in_=k.rearrange("(g c t) h d -> c g t (h d)", g=2, t=4))
+        chunk_order = [2, 3, 4, 5, 6, 7, 1, 0]
+        nc.sync.dma_start(out=q_sb[:, 8:12, :], in_=q_view[:, 8:12, :])
+        nc.sync.dma_start(out=v_sb[:], in_=v.rearrange("(g c t) h d -> c g t (h d)", g=2, t=4))
+        nc.sync.dma_start(out=w_sb[:], in_=W_proj.rearrange("(a p) f -> p a f", p=P))
+        for a in chunk_order[1:]:
+            nc.sync.dma_start(out=q_sb[:, 4 * a:4 * a + 4, :], in_=q_view[:, 4 * a:4 * a + 4, :])
+
+        ident = const.tile([P, P], BF16, name="ident")
+        make_identity(nc, ident[:])
+        maskf = const.tile([P, 4, 4, P], F32, name="maskf")
+        nc.gpsimd.memset(maskf[:], 0.0)
+        nc.gpsimd.affine_select(
+            out=maskf[:], in_=maskf[:], pattern=[[128, 4], [-1, 4], [-4, P]],
+            compare_op=ALU.is_ge, fill=MASK_FILL, base=0, channel_multiplier=1)
+        maskb = const.tile([P, 4, 4 * P], BF16, name="maskb")
+        nc.gpsimd.tensor_copy(out=maskb[:], in_=maskf[:].rearrange("p j t c -> p j (t c)"))
+
+        kT = const.tile([P, H, T], BF16, name="kT")
+        vg = const.tile([P, 2, E, 4], BF16, name="vg", align_bytes=64)
+        vcod = const.tile([P, 2, E], U32, name="vcod", align_bytes=64)
+        vsca = const.tile([P, 2, E], U8, name="vsca", align_bytes=64)
+        wg = const.tile([P, E, 4], BF16, name="wg", align_bytes=64)
+        wcod = const.tile([P, E], U32, name="wcod", align_bytes=64)
+        wsca = const.tile([P, E], U8, name="wsca", align_bytes=64)
+
+        if MANUAL:
+            ctx.enter_context(tc.manual_schedule())
+
+        for h in range(H):
+            pk = ps_t.tile([P, 8 * P], BF16, name="pk", tag="pt")
+            for j in range(8):
+                nc.tensor.transpose(pk[:, j * P:(j + 1) * P], k_sb[:, j // 4, j % 4, h * D:(h + 1) * D], ident[:])
+            if h % 2 == 0:
+                nc.vector.tensor_copy(out=kT[:, h, :], in_=pk[:])
+            else:
+                nc.scalar.copy(out=kT[:, h, :], in_=pk[:])
+
+        n_groups = len(GROUP_ORDER)
+        n_units = 4 * n_groups
+        st = {}
+
+        def passes(i):
+            return 1 if i < 4 else 2
+
+        def live_cols(i, g):
+            if i < 8 and g == i // 4:
+                return 32 * (i % 4 + 1)
+            return P
+
+        def live(ap, i, g):
+            return ap.rearrange("p (t c) -> p t c", t=4)[:, :, 0:live_cols(i, g)]
+
+        def unit(u):
+            return GROUP_ORDER[u // 4], u % 4
+
+        def qt_transposes(gj):
+            i = GROUP_ORDER[gj]
+            pq = ps_o.tile([P, E], BF16, name="pq", tag="o")
+            for h in range(H):
+                nc.tensor.transpose(pq[:, h * P:(h + 1) * P], q_sb[:, i, h * D:(h + 1) * D], ident[:])
+            st[("pq", gj)] = pq
+
+        def qt_copy(gj):
+            qT = work.tile([P, E], BF16, name="qT", tag="qT", bufs=4)
+            nc.vector.tensor_copy(out=qT[:], in_=st[("pq", gj)][:])
+            st[("qT", gj)] = qT
+
+        def scores(u):
+            i, h = unit(u)
+            qT = st[("qT", u // 4)]
+            np_ = passes(i)
+            mx = small.tile([P, 2], F32, name="mx", tag="mx")
+            banks = []
+            for g in range(np_):
+                sg = ps_s.tile([P, 512], F32, name="sg", tag="s")
+                masked = (i < 8) and (g == i // 4)
+                nc.tensor.matmul(sg[:], lhsT=qT[:, h * P:(h + 1) * P], rhs=kT[:, h, g * 512:(g + 1) * 512],
+                                 start=True, stop=not masked)
+                if masked:
+                    nc.tensor.matmul(sg[:], lhsT=ident[:], rhs=maskb[:, i % 4, :], start=False, stop=True)
+                banks.append(sg)
+            for g in range(np_):
+                nc.vector.tensor_reduce(out=mx[:, g:g + 1], in_=live(banks[g][:], i, g), axis=AX.XY, op=ALU.max)
+            nb = small.tile([P, 1], F32, name="nb", tag="nb")
+            if np_ == 2:
+                nc.vector.tensor_scalar(out=nb[:], in0=mx[:, 0:1], scalar1=mx[:, 1:2], scalar2=-SCALE,
+                                        op0=ALU.max, op1=ALU.mult)
+            else:
+                nc.vector.tensor_scalar(out=nb[:], in0=mx[:, 0:1], scalar1=-SCALE, scalar2=None, op0=ALU.mult)
+            st[("s", u)] = banks
+            st[("nb", u)] = nb
+
+        def exps(u):
+            i, h = unit(u)
+            if h == 0:
+                st[("rs", u // 4)] = small.tile([P, H, 2], F32, name="rs", tag="rs")
+            rs = st[("rs", u // 4)]
+            e = work.tile([P, T], BF16, name="e", tag="e")
+            for g in range(passes(i)):
+                eg = e[:, g * 512:(g + 1) * 512]
+                n_live = live_cols(i, g)
+                if n_live < P:
+                    nc.gpsimd.memset(eg.rearrange("p (t c) -> p t c", t=4)[:, :, n_live:P], 0.0)
+                nc.scalar.activation(out=live(eg, i, g), in_=live(st[("s", u)][g][:], i, g), func=ACTF.Exp,
+                                     bias=st[("nb", u)][:], scale=SCALE, accum_out=rs[:, h, g:g + 1])
+            st[("e", u)] = e
+
+        def e_transposes(u):
+            i, h = unit(u)
+            e = st[("e", u)]
+            pt = ps_t.tile([P, 8 * P], BF16, name="pt", tag="pt")
+            for j in range(4 * passes(i)):
+                nc.tensor.transpose(pt[:, j * P:(j + 1) * P], e[:, j * P:(j + 1) * P], ident[:])
+            st[("pt", u)] = pt
+
+        def e_copy(u):
+            i, h = unit(u)
+            np_ = passes(i)
+            gr = work.tile([P, 2, P, 4], BF16, name="gr", tag="gr", align_bytes=64)
+            src = st[("pt", u)][:, 0:np_ * 512].rearrange("p (g t q) -> p g q t", g=np_, t=4)
+            if u % 8 == 5:
+                nc.vector.tensor_copy(out=gr[:, 0:np_], in_=src)
+            else:
+                nc.scalar.copy(out=gr[:, 0:np_], in_=src)
+            st[("gr", u)] = gr
+
+        def e_quant(u):
+            i, h = unit(u)
+            np_ = passes(i)
+            if h == 0:
+                st[("cod", u // 4)] = work.tile([P, H, 2, P], U32, name="cod", tag="cod", align_bytes=64)
+                st[("sca", u // 4)] = work.tile([P, H, 2, P], U8, name="sca", tag="sca", align_bytes=64)
+            cod = st[("cod", u // 4)]
+            sca = st[("sca", u // 4)]
+            nc.vector.quantize_mx(
+                out=cod[:, h, 0:np_, :].rearrange("p g q -> p (g q)").bitcast(FP8X4),
+                scales=sca[:, h, 0:np_, :].rearrange("p g q -> p (g q)"),
+                in_=st[("gr", u)][:, 0:np_].rearrange("p g q t -> p (g q t)"))
+
+        def av(gi):
+            i = GROUP_ORDER[gi]
+            np_ = passes(i)
+            cod = st[("cod", gi)]
+            sca = st[("sca", gi)]
+            o = ps_o.tile([P, E], F32, name="o", tag="o")
+            for h in range(H):
+                for g in range(np_):
+                    nc.tensor.matmul_mx(
+                        out=o[:, h * D:(h + 1) * D],
+                        lhsT=cod[:, h, g, :].bitcast(FP8X4), lhsT_scale=sca[:, h, g, :],
+                        rhs=vcod[:, g, h * D:(h + 1) * D].bitcast(FP8X4), rhs_scale=vsca[:, g, h * D:(h + 1) * D],
+                        start=(g == 0), stop=(g == np_ - 1))
+            st[("o", gi)] = o
+
+        def norm(gi):
+            i = GROUP_ORDER[gi]
+            rs = st[("rs", gi)]
+            rinv = small.tile([P, H], F32, name="rinv", tag="rinv")
+            if passes(i) == 2:
+                rsum = small.tile([P, H], F32, name="rsum", tag="rsum")
+                nc.vector.tensor_reduce(out=rsum[:], in_=rs[:], axis=AX.X, op=ALU.add)
+                nc.vector.reciprocal(out=rinv[:], in_=rsum[:])
+            else:
+                nc.vector.reciprocal(out=rinv[:], in_=rs[:, :, 0])
+            ob = work.tile([P, H, D], BF16, name="ob", tag="ob")
+            nc.vector.tensor_tensor(out=ob[:], in0=st[("o", gi)][:].rearrange("p (h d) -> p h d", h=H),
+                                    in1=rinv[:].unsqueeze(2).to_broadcast([P, H, D]), op=ALU.mult)
+            st[("ob", gi)] = ob
+
+        def o_transposes(gi):
+            ob = st[("ob", gi)]
+            po = ps_m.tile([P, E], BF16, name="po", tag="m")
+            for t in range(4):
+                nc.tensor.transpose(po[:, t * P:(t + 1) * P], ob[:, t, :], ident[:])
+            st[("po", gi)] = po
+
+        def o_copy(gi):
+            og = work.tile([P, P, 4], BF16, name="og", tag="og", align_bytes=64)
+            nc.vector.tensor_copy(out=og[:], in_=st[("po", gi)][:].rearrange("p (t q) -> p q t", t=4))
+            st[("og", gi)] = og
+
+        def o_quant(gi):
+            ocod = work.tile([P, P], U32, name="ocod", tag="ocod", align_bytes=64)
+            osca = work.tile([P, P], U8, name="osca", tag="osca", align_bytes=64)
+            nc.vector.quantize_mx(out=ocod[:].bitcast(FP8X4), scales=osca[:],
+                                  in_=st[("og", gi)][:].rearrange("p q t -> p (q t)"))
+            st[("ocod", gi)] = ocod
+            st[("osca", gi)] = osca
+
+        def proj(gi):
+            y = ps_m.tile([P, E], F32, name="y", tag="m")
+            nc.tensor.matmul_mx(out=y[:], lhsT=st[("ocod", gi)][:].bitcast(FP8X4), lhsT_scale=st[("osca", gi)][:],
+                                rhs=wcod[:].bitcast(FP8X4), rhs_scale=wsca[:], start=True, stop=True)
+            st[("y", gi)] = y
+
+        def y_out(gi):
+            i = GROUP_ORDER[gi]
+            ysb = work.tile([P, E], F32, name="ysb", tag="ysb")
+            nc.vector.tensor_copy(out=ysb[:], in_=st[("y", gi)][:])
+            nc.sync.dma_start(out=out[i * P:(i + 1) * P, :], in_=ysb[:])
+
+        def w_transposes(a):
+            pw = ps_m.tile([P, E], BF16, name="pw", tag="m")
+            for t in range(4):
+                nc.tensor.transpose(pw[:, t * P:(t + 1) * P], w_sb[:, a, t * P:(t + 1) * P], ident[:])
+            st[("pw", a)] = pw
+
+        def w_copy(a):
+            nc.vector.tensor_copy(out=wg[:, a * P:(a + 1) * P, :],
+                                  in_=st[("pw", a)][:].rearrange("p (t o) -> p o t", t=4))
+
+        for s in range(-8, n_units + 12):
+            r = s % 4
+            if r == 1 and 0 <= (s + 7) // 4 < n_groups:
+                qt_copy((s + 7) // 4)
+            if r == 3 and 0 <= (s - 11) // 4 < n_groups:
+                y_out((s - 11) // 4)
+            if r == 0 and 0 <= (s - 8) // 4 < n_groups:
+                o_copy((s - 8) // 4)
+            if 1 <= s <= 4:
+                w_copy(s - 1)
+            if 0 <= s - 1 < n_units:
+                e_copy(s - 1)
+            if 0 <= s + 2 < n_units:
+                scores(s + 2)
+            if 0 <= s + 1 < n_units:
+                exps(s + 1)
+            if 0 <= s < n_units:
+                e_transposes(s)
+            if 0 <= s - 1 < n_units:
+                e_quant(s - 1)
+            if s == -1 or s == 0:
+                g = s + 1
+                nc.vector.tensor_copy(out=vg[:, g], in_=v_sb[:, g].rearrange("p t f -> p f t"))
+            if s == 1 or s == 2:
+                g = s - 1
+                nc.vector.quantize_mx(out=vcod[:, g, :].bitcast(FP8X4), scales=vsca[:, g, :],
+                                      in_=vg[:, g].rearrange("p f t -> p (f t)"))
+            if 0 <= s <= 3:
+                w_transposes(s)
+            if s == 6:
+                nc.vector.quantize_mx(out=wcod[:].bitcast(FP8X4), scales=wsca[:],
+                                      in_=wg[:].rearrange("p o t -> p (o t)"))
+            if r == 0 and 0 <= (s - 8) // 4 < n_groups:
+                o_quant((s - 8) // 4)
+            if r == 1 and 0 <= (s - 5) // 4 < n_groups:
+                av((s - 5) // 4)
+            if r == 1 and 0 <= (s - 9) // 4 < n_groups:
+                proj((s - 9) // 4)
+            if r == 2 and 0 <= (s - 6) // 4 < n_groups:
+                norm((s - 6) // 4)
+            if r == 3 and 0 <= (s - 7) // 4 < n_groups:
+                o_transposes((s - 7) // 4)
+            if r == 0 and 0 <= (s + 8) // 4 < n_groups:
+                qt_transposes((s + 8) // 4)

@@ -106,7 +106,7 @@ def tile_mha_t_kernel(tc, q, k, v, W_proj, out):
 
         def qt_copy(gj):
             qT = work.tile([P, E], BF16, name="qT", tag="qT", bufs=4)
-            nc.vector.tensor_copy(out=qT[:], in_=st[("pq", gj)][:])
+            nc.scalar.copy(out=qT[:], in_=st[("pq", gj)][:])
             st[("qT", gj)] = qT
 
         def scores(u):
@@ -160,26 +160,32 @@ def tile_mha_t_kernel(tc, q, k, v, W_proj, out):
         def e_copy(u):
             i, h = unit(u)
             np_ = passes(i)
-            gr = work.tile([P, 2, P, 4], BF16, name="gr", tag="gr", align_bytes=64)
-            src = st[("pt", u)][:, 0:np_ * 512].rearrange("p (g t q) -> p g q t", g=np_, t=4)
-            if u % 8 == 5:
-                nc.vector.tensor_copy(out=gr[:, 0:np_], in_=src)
-            else:
-                nc.scalar.copy(out=gr[:, 0:np_], in_=src)
-            st[("gr", u)] = gr
-
-        def e_quant(u):
-            i, h = unit(u)
-            np_ = passes(i)
             if h == 0:
-                st[("cod", u // 4)] = work.tile([P, H, 2, P], U32, name="cod", tag="cod", align_bytes=64)
-                st[("sca", u // 4)] = work.tile([P, H, 2, P], U8, name="sca", tag="sca", align_bytes=64)
-            cod = st[("cod", u // 4)]
-            sca = st[("sca", u // 4)]
+                st[("gr", u // 4)] = work.tile([P, H, np_, P, 4], BF16, name="gr", tag="gr", bufs=1, align_bytes=64)
+            gr = st[("gr", u // 4)]
+            pt = st[("pt", u)][:, 0:np_ * 512]
+            if h < 3:
+                tsb = work.tile([P, 8 * P], BF16, name="tsb", tag="tsb")
+                if h == 1:
+                    nc.scalar.copy(out=tsb[:, 0:np_ * 512], in_=pt)
+                else:
+                    nc.vector.tensor_copy(out=tsb[:, 0:np_ * 512], in_=pt)
+                nc.gpsimd.tensor_scalar(
+                    out=gr[:, h], in0=tsb[:, 0:np_ * 512].rearrange("p (g t q) -> p g q t", g=np_, t=4),
+                    scalar1=1.0, scalar2=0.0, op0=ALU.mult, op1=ALU.add)
+            else:
+                nc.scalar.copy(out=gr[:, h], in_=pt.rearrange("p (g t q) -> p g q t", g=np_, t=4))
+
+        def e_quant(gi):
+            np_ = passes(GROUP_ORDER[gi])
+            cod = work.tile([P, H, np_, P], U32, name="cod", tag="cod", align_bytes=64)
+            sca = work.tile([P, H, np_, P], U8, name="sca", tag="sca", align_bytes=64)
             nc.vector.quantize_mx(
-                out=cod[:, h, 0:np_, :].rearrange("p g q -> p (g q)").bitcast(FP8X4),
-                scales=sca[:, h, 0:np_, :].rearrange("p g q -> p (g q)"),
-                in_=st[("gr", u)][:, 0:np_].rearrange("p g q t -> p (g q t)"))
+                out=cod[:].rearrange("p h g q -> p (h g q)").bitcast(FP8X4),
+                scales=sca[:].rearrange("p h g q -> p (h g q)"),
+                in_=st[("gr", gi)][:].rearrange("p h g q t -> p (h g q t)"))
+            st[("cod", gi)] = cod
+            st[("sca", gi)] = sca
 
         def av(gi):
             i = GROUP_ORDER[gi]
@@ -220,7 +226,7 @@ def tile_mha_t_kernel(tc, q, k, v, W_proj, out):
 
         def o_copy(gi):
             og = work.tile([P, P, 4], BF16, name="og", tag="og", align_bytes=64)
-            nc.vector.tensor_copy(out=og[:], in_=st[("po", gi)][:].rearrange("p (t q) -> p q t", t=4))
+            nc.scalar.copy(out=og[:], in_=st[("po", gi)][:].rearrange("p (t q) -> p q t", t=4))
             st[("og", gi)] = og
 
         def o_quant(gi):
@@ -240,7 +246,7 @@ def tile_mha_t_kernel(tc, q, k, v, W_proj, out):
         def y_out(gi):
             i = GROUP_ORDER[gi]
             ysb = work.tile([P, E], F32, name="ysb", tag="ysb")
-            nc.vector.tensor_copy(out=ysb[:], in_=st[("y", gi)][:])
+            nc.scalar.copy(out=ysb[:], in_=st[("y", gi)][:])
             nc.sync.dma_start(out=out[i * P:(i + 1) * P, :], in_=ysb[:])
 
         def w_transposes(a):
@@ -271,8 +277,8 @@ def tile_mha_t_kernel(tc, q, k, v, W_proj, out):
                 exps(s + 1)
             if 0 <= s < n_units:
                 e_transposes(s)
-            if 0 <= s - 1 < n_units:
-                e_quant(s - 1)
+            if 0 <= s - 1 < n_units and (s - 1) % 4 == 3:
+                e_quant((s - 1) // 4)
             if s == -1 or s == 0:
                 g = s + 1
                 nc.vector.tensor_copy(out=vg[:, g], in_=v_sb[:, g].rearrange("p t f -> p f t"))

@@ -31,19 +31,23 @@ def tile_mha_t_kernel(tc, q, k, v, W_proj, out):
         const = ctx.enter_context(tc.tile_pool(name="const", bufs=1))
         work = ctx.enter_context(tc.tile_pool(name="work", bufs=3))
         small = ctx.enter_context(tc.tile_pool(name="small", bufs=4))
-        ps_s = ctx.enter_context(tc.psum_pool(name="ps_s", bufs=4))
-        ps_t = ctx.enter_context(tc.psum_pool(name="ps_t", bufs=2))
-        ps_o = ctx.enter_context(tc.psum_pool(name="ps_o", bufs=1))
-        ps_m = ctx.enter_context(tc.psum_pool(name="ps_m", bufs=1))
+        ps_s = ctx.enter_context(tc.psum_pool(name="ps_s", bufs=5))
+        ps_t = ctx.enter_context(tc.psum_pool(name="ps_x", bufs=3))
+        ps_o = ps_t
+        ps_m = ps_t
 
-        k_sb = const.tile([P, 2, 4, E], BF16, name="k_sb")
+        kv = ctx.enter_context(tc.tile_pool(name="kv", bufs=1))
+        k_sb = kv.tile([P, 2, 4, E], BF16, name="k_sb", tag="kv", align_bytes=64)
         v_sb = const.tile([P, 2, 4, E], BF16, name="v_sb")
         w_sb = const.tile([P, 4, E], BF16, name="w_sb")
         q_sb = const.tile([P, 32, E], BF16, name="q_sb")
         q_view = q.rearrange("(i p) h d -> p i (h d)", p=P)
-        nc.sync.dma_start(out=k_sb[:], in_=k.rearrange("(g c t) h d -> c g t (h d)", g=2, t=4))
+        k_view = k.rearrange("(g c t) h d -> c g t (h d)", g=2, t=4)
         chunk_order = [2, 3, 4, 5, 6, 7, 1, 0]
-        nc.sync.dma_start(out=q_sb[:, 8:12, :], in_=q_view[:, 8:12, :])
+        nc.sync.dma_start(out=k_sb[:, 0], in_=k_view[:, 0])
+        nc.sync.dma_start(out=q_sb[:, 8:9, :], in_=q_view[:, 8:9, :])
+        nc.sync.dma_start(out=k_sb[:, 1], in_=k_view[:, 1])
+        nc.sync.dma_start(out=q_sb[:, 9:12, :], in_=q_view[:, 9:12, :])
         nc.sync.dma_start(out=v_sb[:], in_=v.rearrange("(g c t) h d -> c g t (h d)", g=2, t=4))
         nc.sync.dma_start(out=w_sb[:], in_=W_proj.rearrange("(a p) f -> p a f", p=P))
         for a in chunk_order[1:]:
@@ -60,7 +64,6 @@ def tile_mha_t_kernel(tc, q, k, v, W_proj, out):
         nc.gpsimd.tensor_copy(out=maskb[:], in_=maskf[:].rearrange("p j t c -> p j (t c)"))
 
         kT = const.tile([P, H, T], BF16, name="kT")
-        vg = const.tile([P, 2, E, 4], BF16, name="vg", align_bytes=64)
         vcod = const.tile([P, 2, E], U32, name="vcod", align_bytes=64)
         vsca = const.tile([P, 2, E], U8, name="vsca", align_bytes=64)
         wg = const.tile([P, E, 4], BF16, name="wg", align_bytes=64)
@@ -70,14 +73,23 @@ def tile_mha_t_kernel(tc, q, k, v, W_proj, out):
         if MANUAL:
             ctx.enter_context(tc.manual_schedule())
 
-        for h in range(H):
-            pk = ps_t.tile([P, 8 * P], BF16, name="pk", tag="pt")
+        def kt_prep(g, hp):
+            pk = ps_t.tile([P, 8 * P], BF16, name="pk", tag="x")
             for j in range(8):
-                nc.tensor.transpose(pk[:, j * P:(j + 1) * P], k_sb[:, j // 4, j % 4, h * D:(h + 1) * D], ident[:])
-            if h % 2 == 0:
-                nc.vector.tensor_copy(out=kT[:, h, :], in_=pk[:])
+                h = 2 * hp + j // 4
+                nc.tensor.transpose(pk[:, j * P:(j + 1) * P], k_sb[:, g, j % 4, h * D:(h + 1) * D], ident[:])
+            dst = kT[:, 2 * hp:2 * hp + 2, g * 512:(g + 1) * 512]
+            src = pk[:].rearrange("p (h n) -> p h n", h=2)
+            if g == 0:
+                nc.vector.tensor_copy(out=dst, in_=src)
             else:
-                nc.scalar.copy(out=kT[:, h, :], in_=pk[:])
+                nc.scalar.copy(out=dst, in_=src)
+
+        kt_prep(0, 0)
+        kt_prep(1, 0)
+        kt_prep(0, 1)
+        kt_prep(1, 1)
+        vg = kv.tile([P, 2, E, 4], BF16, name="vg", tag="kv", align_bytes=64)
 
         n_groups = len(GROUP_ORDER)
         n_units = 4 * n_groups
@@ -99,14 +111,14 @@ def tile_mha_t_kernel(tc, q, k, v, W_proj, out):
 
         def qt_transposes(gj):
             i = GROUP_ORDER[gj]
-            pq = ps_o.tile([P, E], BF16, name="pq", tag="o")
+            pq = ps_o.tile([P, E], BF16, name="pq", tag="x")
             for h in range(H):
                 nc.tensor.transpose(pq[:, h * P:(h + 1) * P], q_sb[:, i, h * D:(h + 1) * D], ident[:])
             st[("pq", gj)] = pq
 
         def qt_copy(gj):
             qT = work.tile([P, E], BF16, name="qT", tag="qT", bufs=4)
-            nc.scalar.copy(out=qT[:], in_=st[("pq", gj)][:])
+            nc.any.tensor_copy(out=qT[:], in_=st[("pq", gj)][:])
             st[("qT", gj)] = qT
 
         def scores(u):
@@ -152,7 +164,7 @@ def tile_mha_t_kernel(tc, q, k, v, W_proj, out):
         def e_transposes(u):
             i, h = unit(u)
             e = st[("e", u)]
-            pt = ps_t.tile([P, 8 * P], BF16, name="pt", tag="pt")
+            pt = ps_t.tile([P, 8 * P], BF16, name="pt", tag="x")
             for j in range(4 * passes(i)):
                 nc.tensor.transpose(pt[:, j * P:(j + 1) * P], e[:, j * P:(j + 1) * P], ident[:])
             st[("pt", u)] = pt
@@ -160,39 +172,30 @@ def tile_mha_t_kernel(tc, q, k, v, W_proj, out):
         def e_copy(u):
             i, h = unit(u)
             np_ = passes(i)
-            if h == 0:
-                st[("gr", u // 4)] = work.tile([P, H, np_, P, 4], BF16, name="gr", tag="gr", bufs=1, align_bytes=64)
-            gr = st[("gr", u // 4)]
-            pt = st[("pt", u)][:, 0:np_ * 512]
-            if h < 3:
-                tsb = work.tile([P, 8 * P], BF16, name="tsb", tag="tsb")
-                if h == 1:
-                    nc.scalar.copy(out=tsb[:, 0:np_ * 512], in_=pt)
-                else:
-                    nc.vector.tensor_copy(out=tsb[:, 0:np_ * 512], in_=pt)
-                nc.gpsimd.tensor_scalar(
-                    out=gr[:, h], in0=tsb[:, 0:np_ * 512].rearrange("p (g t q) -> p g q t", g=np_, t=4),
-                    scalar1=1.0, scalar2=0.0, op0=ALU.mult, op1=ALU.add)
-            else:
-                nc.scalar.copy(out=gr[:, h], in_=pt.rearrange("p (g t q) -> p g q t", g=np_, t=4))
+            gr = work.tile([P, 2, P, 4], BF16, name="gr", tag="gr", align_bytes=64)
+            src = st[("pt", u)][:, 0:np_ * 512].rearrange("p (g t q) -> p g q t", g=np_, t=4)
+            nc.any.tensor_copy(out=gr[:, 0:np_], in_=src)
+            st[("gr", u)] = gr
 
-        def e_quant(gi):
-            np_ = passes(GROUP_ORDER[gi])
-            cod = work.tile([P, H, np_, P], U32, name="cod", tag="cod", align_bytes=64)
-            sca = work.tile([P, H, np_, P], U8, name="sca", tag="sca", align_bytes=64)
+        def e_quant(u):
+            i, h = unit(u)
+            np_ = passes(i)
+            if h == 0:
+                st[("cod", u // 4)] = work.tile([P, H, 2, P], U32, name="cod", tag="cod", align_bytes=64)
+                st[("sca", u // 4)] = work.tile([P, H, 2, P], U8, name="sca", tag="sca", align_bytes=64)
+            cod = st[("cod", u // 4)]
+            sca = st[("sca", u // 4)]
             nc.vector.quantize_mx(
-                out=cod[:].rearrange("p h g q -> p (h g q)").bitcast(FP8X4),
-                scales=sca[:].rearrange("p h g q -> p (h g q)"),
-                in_=st[("gr", gi)][:].rearrange("p h g q t -> p (h g q t)"))
-            st[("cod", gi)] = cod
-            st[("sca", gi)] = sca
+                out=cod[:, h, 0:np_, :].rearrange("p g q -> p (g q)").bitcast(FP8X4),
+                scales=sca[:, h, 0:np_, :].rearrange("p g q -> p (g q)"),
+                in_=st[("gr", u)][:, 0:np_].rearrange("p g q t -> p (g q t)"))
 
         def av(gi):
             i = GROUP_ORDER[gi]
             np_ = passes(i)
             cod = st[("cod", gi)]
             sca = st[("sca", gi)]
-            o = ps_o.tile([P, E], F32, name="o", tag="o")
+            o = ps_o.tile([P, E], F32, name="o", tag="x")
             for h in range(H):
                 for g in range(np_):
                     nc.tensor.matmul_mx(
@@ -219,14 +222,14 @@ def tile_mha_t_kernel(tc, q, k, v, W_proj, out):
 
         def o_transposes(gi):
             ob = st[("ob", gi)]
-            po = ps_m.tile([P, E], BF16, name="po", tag="m")
+            po = ps_m.tile([P, E], BF16, name="po", tag="x")
             for t in range(4):
                 nc.tensor.transpose(po[:, t * P:(t + 1) * P], ob[:, t, :], ident[:])
             st[("po", gi)] = po
 
         def o_copy(gi):
             og = work.tile([P, P, 4], BF16, name="og", tag="og", align_bytes=64)
-            nc.scalar.copy(out=og[:], in_=st[("po", gi)][:].rearrange("p (t q) -> p q t", t=4))
+            nc.any.tensor_copy(out=og[:], in_=st[("po", gi)][:].rearrange("p (t q) -> p q t", t=4))
             st[("og", gi)] = og
 
         def o_quant(gi):
@@ -238,7 +241,7 @@ def tile_mha_t_kernel(tc, q, k, v, W_proj, out):
             st[("osca", gi)] = osca
 
         def proj(gi):
-            y = ps_m.tile([P, E], F32, name="y", tag="m")
+            y = ps_m.tile([P, E], F32, name="y", tag="x")
             nc.tensor.matmul_mx(out=y[:], lhsT=st[("ocod", gi)][:].bitcast(FP8X4), lhsT_scale=st[("osca", gi)][:],
                                 rhs=wcod[:].bitcast(FP8X4), rhs_scale=wsca[:], start=True, stop=True)
             st[("y", gi)] = y
@@ -246,11 +249,11 @@ def tile_mha_t_kernel(tc, q, k, v, W_proj, out):
         def y_out(gi):
             i = GROUP_ORDER[gi]
             ysb = work.tile([P, E], F32, name="ysb", tag="ysb")
-            nc.scalar.copy(out=ysb[:], in_=st[("y", gi)][:])
+            nc.any.tensor_copy(out=ysb[:], in_=st[("y", gi)][:])
             nc.sync.dma_start(out=out[i * P:(i + 1) * P, :], in_=ysb[:])
 
         def w_transposes(a):
-            pw = ps_m.tile([P, E], BF16, name="pw", tag="m")
+            pw = ps_m.tile([P, E], BF16, name="pw", tag="x")
             for t in range(4):
                 nc.tensor.transpose(pw[:, t * P:(t + 1) * P], w_sb[:, a, t * P:(t + 1) * P], ident[:])
             st[("pw", a)] = pw
@@ -277,8 +280,8 @@ def tile_mha_t_kernel(tc, q, k, v, W_proj, out):
                 exps(s + 1)
             if 0 <= s < n_units:
                 e_transposes(s)
-            if 0 <= s - 1 < n_units and (s - 1) % 4 == 3:
-                e_quant((s - 1) // 4)
+            if 0 <= s - 1 < n_units:
+                e_quant(s - 1)
             if s == -1 or s == 0:
                 g = s + 1
                 nc.vector.tensor_copy(out=vg[:, g], in_=v_sb[:, g].rearrange("p t f -> p f t"))

@@ -9,6 +9,7 @@ E = H * D
 FLOPS = 2 * S * T * D * H + 2 * (512 * 512 + 3584 * 1024) * D * H + 2 * S * E * E
 
 MANUAL = False
+E_COPY_ON_VECTOR = (1, 4)
 
 BF16 = mybir.dt.bfloat16
 F32 = mybir.dt.float32
@@ -29,8 +30,8 @@ def tile_mha_t_kernel(tc, q, k, v, W_proj, out):
     nc = tc.nc
     with ExitStack() as ctx:
         const = ctx.enter_context(tc.tile_pool(name="const", bufs=1))
-        work = ctx.enter_context(tc.tile_pool(name="work", bufs=3))
-        small = ctx.enter_context(tc.tile_pool(name="small", bufs=4))
+        work = ctx.enter_context(tc.tile_pool(name="work", bufs=4))
+        small = ctx.enter_context(tc.tile_pool(name="small", bufs=6))
         ps_s = ctx.enter_context(tc.psum_pool(name="ps_s", bufs=5))
         ps_t = ctx.enter_context(tc.psum_pool(name="ps_x", bufs=3))
         ps_o = ps_t
@@ -118,7 +119,7 @@ def tile_mha_t_kernel(tc, q, k, v, W_proj, out):
 
         def qt_copy(gj):
             qT = work.tile([P, E], BF16, name="qT", tag="qT", bufs=4)
-            nc.any.tensor_copy(out=qT[:], in_=st[("pq", gj)][:])
+            nc.vector.tensor_copy(out=qT[:], in_=st[("pq", gj)][:])
             st[("qT", gj)] = qT
 
         def scores(u):
@@ -174,7 +175,10 @@ def tile_mha_t_kernel(tc, q, k, v, W_proj, out):
             np_ = passes(i)
             gr = work.tile([P, 2, P, 4], BF16, name="gr", tag="gr", align_bytes=64)
             src = st[("pt", u)][:, 0:np_ * 512].rearrange("p (g t q) -> p g q t", g=np_, t=4)
-            nc.any.tensor_copy(out=gr[:, 0:np_], in_=src)
+            if u % 7 in E_COPY_ON_VECTOR:
+                nc.vector.tensor_copy(out=gr[:, 0:np_], in_=src)
+            else:
+                nc.scalar.copy(out=gr[:, 0:np_], in_=src)
             st[("gr", u)] = gr
 
         def e_quant(u):
@@ -229,7 +233,7 @@ def tile_mha_t_kernel(tc, q, k, v, W_proj, out):
 
         def o_copy(gi):
             og = work.tile([P, P, 4], BF16, name="og", tag="og", align_bytes=64)
-            nc.any.tensor_copy(out=og[:], in_=st[("po", gi)][:].rearrange("p (t q) -> p q t", t=4))
+            nc.scalar.copy(out=og[:], in_=st[("po", gi)][:].rearrange("p (t q) -> p q t", t=4))
             st[("og", gi)] = og
 
         def o_quant(gi):
@@ -249,7 +253,7 @@ def tile_mha_t_kernel(tc, q, k, v, W_proj, out):
         def y_out(gi):
             i = GROUP_ORDER[gi]
             ysb = work.tile([P, E], F32, name="ysb", tag="ysb")
-            nc.any.tensor_copy(out=ysb[:], in_=st[("y", gi)][:])
+            nc.scalar.copy(out=ysb[:], in_=st[("y", gi)][:])
             nc.sync.dma_start(out=out[i * P:(i + 1) * P, :], in_=ysb[:])
 
         def w_transposes(a):

@@ -9,7 +9,6 @@ E = H * D
 FLOPS = 2 * S * T * D * H + 2 * (512 * 512 + 3584 * 1024) * D * H + 2 * S * E * E
 
 MANUAL = False
-E_COPY_ON_VECTOR = (1, 4)
 
 BF16 = mybir.dt.bfloat16
 F32 = mybir.dt.float32
@@ -57,12 +56,12 @@ def tile_mha_t_kernel(tc, q, k, v, W_proj, out):
         ident = const.tile([P, P], BF16, name="ident")
         make_identity(nc, ident[:])
         maskf = const.tile([P, 4, 4, P], F32, name="maskf")
-        nc.gpsimd.memset(maskf[:], 0.0)
+        nc.vector.memset(maskf[:], 0.0)
         nc.gpsimd.affine_select(
             out=maskf[:], in_=maskf[:], pattern=[[128, 4], [-1, 4], [-4, P]],
             compare_op=ALU.is_ge, fill=MASK_FILL, base=0, channel_multiplier=1)
         maskb = const.tile([P, 4, 4 * P], BF16, name="maskb")
-        nc.gpsimd.tensor_copy(out=maskb[:], in_=maskf[:].rearrange("p j t c -> p j (t c)"))
+        nc.vector.tensor_copy(out=maskb[:], in_=maskf[:].rearrange("p j t c -> p j (t c)"))
 
         kT = const.tile([P, H, T], BF16, name="kT")
         vcod = const.tile([P, 2, E], U32, name="vcod", align_bytes=64)
@@ -140,10 +139,11 @@ def tile_mha_t_kernel(tc, q, k, v, W_proj, out):
                 nc.vector.tensor_reduce(out=mx[:, g:g + 1], in_=live(banks[g][:], i, g), axis=AX.XY, op=ALU.max)
             nb = small.tile([P, 1], F32, name="nb", tag="nb")
             if np_ == 2:
-                nc.vector.tensor_scalar(out=nb[:], in0=mx[:, 0:1], scalar1=mx[:, 1:2], scalar2=-SCALE,
+                nc.gpsimd.tensor_scalar(out=nb[:], in0=mx[:, 0:1], scalar1=mx[:, 1:2], scalar2=-SCALE,
                                         op0=ALU.max, op1=ALU.mult)
             else:
-                nc.vector.tensor_scalar(out=nb[:], in0=mx[:, 0:1], scalar1=-SCALE, scalar2=None, op0=ALU.mult)
+                nc.gpsimd.tensor_scalar(out=nb[:], in0=mx[:, 0:1], scalar1=-SCALE, scalar2=0.0,
+                                        op0=ALU.mult, op1=ALU.add)
             st[("s", u)] = banks
             st[("nb", u)] = nb
 
@@ -173,26 +173,24 @@ def tile_mha_t_kernel(tc, q, k, v, W_proj, out):
         def e_copy(u):
             i, h = unit(u)
             np_ = passes(i)
-            gr = work.tile([P, 2, P, 4], BF16, name="gr", tag="gr", align_bytes=64)
+            if h % 2 == 0:
+                st[("gr", u // 2)] = work.tile([P, 2, np_, P, 4], BF16, name="gr", tag="gr", align_bytes=64)
+            gr = st[("gr", u // 2)]
             src = st[("pt", u)][:, 0:np_ * 512].rearrange("p (g t q) -> p g q t", g=np_, t=4)
-            if u % 7 in E_COPY_ON_VECTOR:
-                nc.vector.tensor_copy(out=gr[:, 0:np_], in_=src)
-            else:
-                nc.scalar.copy(out=gr[:, 0:np_], in_=src)
-            st[("gr", u)] = gr
+            nc.any.tensor_copy(out=gr[:, h % 2], in_=src)
 
         def e_quant(u):
             i, h = unit(u)
             np_ = passes(i)
-            if h == 0:
-                st[("cod", u // 4)] = work.tile([P, H, 2, P], U32, name="cod", tag="cod", align_bytes=64)
-                st[("sca", u // 4)] = work.tile([P, H, 2, P], U8, name="sca", tag="sca", align_bytes=64)
+            if h == 1:
+                st[("cod", u // 4)] = work.tile([P, H, np_, P], U32, name="cod", tag="cod", align_bytes=64)
+                st[("sca", u // 4)] = work.tile([P, H, np_, P], U8, name="sca", tag="sca", align_bytes=64)
             cod = st[("cod", u // 4)]
             sca = st[("sca", u // 4)]
             nc.vector.quantize_mx(
-                out=cod[:, h, 0:np_, :].rearrange("p g q -> p (g q)").bitcast(FP8X4),
-                scales=sca[:, h, 0:np_, :].rearrange("p g q -> p (g q)"),
-                in_=st[("gr", u)][:, 0:np_].rearrange("p g q t -> p (g q t)"))
+                out=cod[:, h - 1:h + 1].rearrange("p h g q -> p (h g q)").bitcast(FP8X4),
+                scales=sca[:, h - 1:h + 1].rearrange("p h g q -> p (h g q)"),
+                in_=st[("gr", u // 2)][:].rearrange("p h g q t -> p (h g q t)"))
 
         def av(gi):
             i = GROUP_ORDER[gi]
@@ -215,7 +213,7 @@ def tile_mha_t_kernel(tc, q, k, v, W_proj, out):
             rinv = small.tile([P, H], F32, name="rinv", tag="rinv")
             if passes(i) == 2:
                 rsum = small.tile([P, H], F32, name="rsum", tag="rsum")
-                nc.vector.tensor_reduce(out=rsum[:], in_=rs[:], axis=AX.X, op=ALU.add)
+                nc.gpsimd.tensor_tensor(out=rsum[:], in0=rs[:, :, 0], in1=rs[:, :, 1], op=ALU.add)
                 nc.vector.reciprocal(out=rinv[:], in_=rsum[:])
             else:
                 nc.vector.reciprocal(out=rinv[:], in_=rs[:, :, 0])
@@ -233,7 +231,7 @@ def tile_mha_t_kernel(tc, q, k, v, W_proj, out):
 
         def o_copy(gi):
             og = work.tile([P, P, 4], BF16, name="og", tag="og", align_bytes=64)
-            nc.scalar.copy(out=og[:], in_=st[("po", gi)][:].rearrange("p (t q) -> p q t", t=4))
+            nc.any.tensor_copy(out=og[:], in_=st[("po", gi)][:].rearrange("p (t q) -> p q t", t=4))
             st[("og", gi)] = og
 
         def o_quant(gi):
@@ -253,7 +251,7 @@ def tile_mha_t_kernel(tc, q, k, v, W_proj, out):
         def y_out(gi):
             i = GROUP_ORDER[gi]
             ysb = work.tile([P, E], F32, name="ysb", tag="ysb")
-            nc.scalar.copy(out=ysb[:], in_=st[("y", gi)][:])
+            nc.any.tensor_copy(out=ysb[:], in_=st[("y", gi)][:])
             nc.sync.dma_start(out=out[i * P:(i + 1) * P, :], in_=ysb[:])
 
         def w_transposes(a):
@@ -284,7 +282,7 @@ def tile_mha_t_kernel(tc, q, k, v, W_proj, out):
                 exps(s + 1)
             if 0 <= s < n_units:
                 e_transposes(s)
-            if 0 <= s - 1 < n_units:
+            if 0 <= s - 1 < n_units and (s - 1) % 2 == 1:
                 e_quant(s - 1)
             if s == -1 or s == 0:
                 g = s + 1

@@ -31,8 +31,8 @@ def tile_mha_t_kernel(tc, q, k, v, W_proj, out):
         const = ctx.enter_context(tc.tile_pool(name="const", bufs=1))
         work = ctx.enter_context(tc.tile_pool(name="work", bufs=4))
         small = ctx.enter_context(tc.tile_pool(name="small", bufs=6))
-        ps_s = ctx.enter_context(tc.psum_pool(name="ps_s", bufs=5))
-        ps_t = ctx.enter_context(tc.psum_pool(name="ps_x", bufs=3))
+        ps_s = ctx.enter_context(tc.psum_pool(name="ps_s", bufs=4))
+        ps_t = ctx.enter_context(tc.psum_pool(name="ps_x", bufs=4))
         ps_o = ps_t
         ps_m = ps_t
 

@@ -55,15 +55,18 @@ def tile_mha_t_kernel(tc, q, k, v, W_proj, out):
 
         ident = const.tile([P, P], BF16, name="ident")
         make_identity(nc, ident[:])
+        ident_w = const.tile([P, P], F32, name="ident_w")
+        make_identity(nc, ident_w[:])
         maskf = const.tile([P, 4, 4, P], F32, name="maskf")
         nc.vector.memset(maskf[:], 0.0)
         nc.gpsimd.affine_select(
             out=maskf[:], in_=maskf[:], pattern=[[128, 4], [-1, 4], [-4, P]],
             compare_op=ALU.is_ge, fill=MASK_FILL, base=0, channel_multiplier=1)
         maskb = const.tile([P, 4, 4 * P], BF16, name="maskb")
-        nc.vector.tensor_copy(out=maskb[:], in_=maskf[:].rearrange("p j t c -> p j (t c)"))
+        nc.vector.tensor_copy(out=maskb[:].rearrange("p j (u c e) -> p (j u) c e", u=2, e=2),
+                              in_=maskf[:].rearrange("p j (u e) c -> p (j u) c e", u=2))
 
-        kT = const.tile([P, H, T], BF16, name="kT")
+        kT = const.tile([P, 2, H, 512], BF16, name="kT")
         vcod = const.tile([P, 2, E], U32, name="vcod", align_bytes=64)
         vsca = const.tile([P, 2, E], U8, name="vsca", align_bytes=64)
         wg = const.tile([P, E, 4], BF16, name="wg", align_bytes=64)
@@ -78,8 +81,8 @@ def tile_mha_t_kernel(tc, q, k, v, W_proj, out):
             for j in range(8):
                 h = 2 * hp + j // 4
                 nc.tensor.transpose(pk[:, j * P:(j + 1) * P], k_sb[:, g, j % 4, h * D:(h + 1) * D], ident[:])
-            dst = kT[:, 2 * hp:2 * hp + 2, g * 512:(g + 1) * 512]
-            src = pk[:].rearrange("p (h n) -> p h n", h=2)
+            dst = kT[:, g, 2 * hp:2 * hp + 2, :].rearrange("p h (u c e) -> p (h u) c e", u=2, e=2)
+            src = pk[:].rearrange("p (a e c) -> p a c e", a=4, e=2)
             if g == 0:
                 nc.vector.tensor_copy(out=dst, in_=src)
             else:
@@ -104,7 +107,7 @@ def tile_mha_t_kernel(tc, q, k, v, W_proj, out):
             return P
 
         def live(ap, i, g):
-            return ap.rearrange("p (t c) -> p t c", t=4)[:, :, 0:live_cols(i, g)]
+            return ap.rearrange("p (u w) -> p u w", u=2)[:, :, 0:2 * live_cols(i, g)]
 
         def unit(u):
             return GROUP_ORDER[u // 4], u % 4
@@ -130,7 +133,7 @@ def tile_mha_t_kernel(tc, q, k, v, W_proj, out):
             for g in range(np_):
                 sg = ps_s.tile([P, 512], F32, name="sg", tag="s")
                 masked = (i < 8) and (g == i // 4)
-                nc.tensor.matmul(sg[:], lhsT=qT[:, h * P:(h + 1) * P], rhs=kT[:, h, g * 512:(g + 1) * 512],
+                nc.tensor.matmul(sg[:], lhsT=qT[:, h * P:(h + 1) * P], rhs=kT[:, g, h, :],
                                  start=True, stop=not masked)
                 if masked:
                     nc.tensor.matmul(sg[:], lhsT=ident[:], rhs=maskb[:, i % 4, :], start=False, stop=True)
@@ -157,7 +160,7 @@ def tile_mha_t_kernel(tc, q, k, v, W_proj, out):
                 eg = e[:, g * 512:(g + 1) * 512]
                 n_live = live_cols(i, g)
                 if n_live < P:
-                    nc.gpsimd.memset(eg.rearrange("p (t c) -> p t c", t=4)[:, :, n_live:P], 0.0)
+                    nc.gpsimd.memset(eg.rearrange("p (u w) -> p u w", u=2)[:, :, 2 * n_live:2 * P], 0.0)
                 nc.scalar.activation(out=live(eg, i, g), in_=live(st[("s", u)][g][:], i, g), func=ACTF.Exp,
                                      bias=st[("nb", u)][:], scale=SCALE, accum_out=rs[:, h, g:g + 1])
             st[("e", u)] = e
@@ -165,19 +168,20 @@ def tile_mha_t_kernel(tc, q, k, v, W_proj, out):
         def e_transposes(u):
             i, h = unit(u)
             e = st[("e", u)]
-            pt = ps_t.tile([P, 8 * P], BF16, name="pt", tag="x")
-            for j in range(4 * passes(i)):
-                nc.tensor.transpose(pt[:, j * P:(j + 1) * P], e[:, j * P:(j + 1) * P], ident[:])
+            words = e[:].bitcast(F32)
+            pt = ps_t.tile([P, 4 * P], F32, name="pt", tag="x")
+            for j in range(2 * passes(i)):
+                nc.tensor.transpose(pt[:, j * P:(j + 1) * P], words[:, j * P:(j + 1) * P], ident_w[:])
             st[("pt", u)] = pt
 
         def e_copy(u):
             i, h = unit(u)
             np_ = passes(i)
             if h % 2 == 0:
-                st[("gr", u // 2)] = work.tile([P, 2, np_, P, 4], BF16, name="gr", tag="gr", align_bytes=64)
+                st[("gr", u // 2)] = work.tile([P, 2, np_, P, 2], F32, name="gr", tag="gr", align_bytes=64)
             gr = st[("gr", u // 2)]
-            src = st[("pt", u)][:, 0:np_ * 512].rearrange("p (g t q) -> p g q t", g=np_, t=4)
-            nc.any.tensor_copy(out=gr[:, h % 2], in_=src)
+            src = st[("pt", u)][:, 0:np_ * 256].rearrange("p (g u q) -> p g q u", g=np_, u=2)
+            nc.scalar.copy(out=gr[:, h % 2], in_=src)
 
         def e_quant(u):
             i, h = unit(u)
@@ -190,7 +194,7 @@ def tile_mha_t_kernel(tc, q, k, v, W_proj, out):
             nc.vector.quantize_mx(
                 out=cod[:, h - 1:h + 1].rearrange("p h g q -> p (h g q)").bitcast(FP8X4),
                 scales=sca[:, h - 1:h + 1].rearrange("p h g q -> p (h g q)"),
-                in_=st[("gr", u // 2)][:].rearrange("p h g q t -> p (h g q t)"))
+                in_=st[("gr", u // 2)][:].rearrange("p h g q u -> p (h g q u)").bitcast(BF16))
 
         def av(gi):
             i = GROUP_ORDER[gi]

@@ -8,8 +8,6 @@ S, T, H, D = 4096, 1024, 4, 128
 E = H * D
 FLOPS = 2 * S * T * D * H + 2 * (512 * 512 + 3584 * 1024) * D * H + 2 * S * E * E
 
-MANUAL = False
-
 BF16 = mybir.dt.bfloat16
 F32 = mybir.dt.float32
 U32 = mybir.dt.uint32
@@ -31,13 +29,11 @@ def tile_mha_t_kernel(tc, q, k, v, W_proj, out):
         const = ctx.enter_context(tc.tile_pool(name="const", bufs=1))
         work = ctx.enter_context(tc.tile_pool(name="work", bufs=4))
         small = ctx.enter_context(tc.tile_pool(name="small", bufs=6))
-        ps_s = ctx.enter_context(tc.psum_pool(name="ps_s", bufs=4))
-        ps_t = ctx.enter_context(tc.psum_pool(name="ps_x", bufs=4))
-        ps_o = ps_t
-        ps_m = ps_t
+        ps_s = ctx.enter_context(tc.psum_pool(name="ps_s", bufs=6))
+        ps_t = ctx.enter_context(tc.psum_pool(name="ps_t", bufs=1))
+        ps_g = ctx.enter_context(tc.psum_pool(name="ps_g", bufs=1))
 
-        kv = ctx.enter_context(tc.tile_pool(name="kv", bufs=1))
-        k_sb = kv.tile([P, 2, 4, E], BF16, name="k_sb", tag="kv", align_bytes=64)
+        k_sb = const.tile([P, 2, 4, E], BF16, name="k_sb")
         v_sb = const.tile([P, 2, 4, E], BF16, name="v_sb")
         w_sb = const.tile([P, 4, E], BF16, name="w_sb")
         q_sb = const.tile([P, 32, E], BF16, name="q_sb")
@@ -57,46 +53,43 @@ def tile_mha_t_kernel(tc, q, k, v, W_proj, out):
         make_identity(nc, ident[:])
         ident_w = const.tile([P, P], F32, name="ident_w")
         make_identity(nc, ident_w[:])
-        maskf = const.tile([P, 4, 4, P], F32, name="maskf")
-        nc.vector.memset(maskf[:], 0.0)
-        nc.gpsimd.affine_select(
-            out=maskf[:], in_=maskf[:], pattern=[[128, 4], [-1, 4], [-4, P]],
-            compare_op=ALU.is_ge, fill=MASK_FILL, base=0, channel_multiplier=1)
         maskb = const.tile([P, 4, 4 * P], BF16, name="maskb")
-        nc.vector.tensor_copy(out=maskb[:].rearrange("p j (u c e) -> p (j u) c e", u=2, e=2),
-                              in_=maskf[:].rearrange("p j (u e) c -> p (j u) c e", u=2))
+        nc.gpsimd.memset(maskb[:], 0.0)
 
         kT = const.tile([P, 2, H, 512], BF16, name="kT")
+        vg = const.tile([P, 2, E, 4], BF16, name="vg", align_bytes=64)
         vcod = const.tile([P, 2, E], U32, name="vcod", align_bytes=64)
         vsca = const.tile([P, 2, E], U8, name="vsca", align_bytes=64)
-        wg = const.tile([P, E, 4], BF16, name="wg", align_bytes=64)
+        wg = const.tile([P, E, 2], F32, name="wg", align_bytes=64)
         wcod = const.tile([P, E], U32, name="wcod", align_bytes=64)
         wsca = const.tile([P, E], U8, name="wsca", align_bytes=64)
+        warm = const.tile([P, 1], F32, name="warm")
+        nc.vector.memset(warm[:], 0.0)
+        warm_out = const.tile([P, 1], F32, name="warm_out")
 
-        if MANUAL:
-            ctx.enter_context(tc.manual_schedule())
-
-        def kt_prep(g, hp):
-            pk = ps_t.tile([P, 8 * P], BF16, name="pk", tag="x")
-            for j in range(8):
-                h = 2 * hp + j // 4
-                nc.tensor.transpose(pk[:, j * P:(j + 1) * P], k_sb[:, g, j % 4, h * D:(h + 1) * D], ident[:])
-            dst = kT[:, g, 2 * hp:2 * hp + 2, :].rearrange("p h (u c e) -> p (h u) c e", u=2, e=2)
-            src = pk[:].rearrange("p (a e c) -> p a c e", a=4, e=2)
-            if g == 0:
-                nc.vector.tensor_copy(out=dst, in_=src)
-            else:
-                nc.scalar.copy(out=dst, in_=src)
-
-        kt_prep(0, 0)
-        kt_prep(1, 0)
-        kt_prep(0, 1)
-        kt_prep(1, 1)
-        vg = kv.tile([P, 2, E, 4], BF16, name="vg", tag="kv", align_bytes=64)
+        ctx.enter_context(tc.manual_schedule())
+        nc.scalar.activation(out=warm_out[:], in_=warm[:], func=ACTF.Exp)
 
         n_groups = len(GROUP_ORDER)
         n_units = 4 * n_groups
         st = {}
+
+        def mask_select(j):
+            sel = maskb[:, j, :].rearrange("p (u c e) -> p u c e", u=2, e=2)
+            nc.gpsimd.affine_select(
+                out=sel, in_=sel, pattern=[[-2, 2], [-4, P], [-1, 2]],
+                compare_op=ALU.is_ge, fill=MASK_FILL, base=128 * j, channel_multiplier=1)
+
+        def kt_transposes(g, h):
+            pk = ps_s.tile([P, 512], BF16, name="pk", tag="s")
+            for t in range(4):
+                nc.tensor.transpose(pk[:, t * P:(t + 1) * P], k_sb[:, g, t, h * D:(h + 1) * D], ident[:])
+            dst = kT[:, g, h, :].rearrange("p (u c e) -> p u c e", u=2, e=2)
+            src = pk[:].rearrange("p (u e c) -> p u c e", u=2, e=2)
+            if g == 0:
+                nc.vector.tensor_copy(out=dst, in_=src)
+            else:
+                nc.scalar.copy(out=dst, in_=src)
 
         def passes(i):
             return 1 if i < 4 else 2
@@ -114,23 +107,21 @@ def tile_mha_t_kernel(tc, q, k, v, W_proj, out):
 
         def qt_transposes(gj):
             i = GROUP_ORDER[gj]
-            pq = ps_o.tile([P, E], BF16, name="pq", tag="x")
+            pq = ps_g.tile([P, E], BF16, name="pq", tag="g")
             for h in range(H):
                 nc.tensor.transpose(pq[:, h * P:(h + 1) * P], q_sb[:, i, h * D:(h + 1) * D], ident[:])
             st[("pq", gj)] = pq
 
         def qt_copy(gj):
-            qT = work.tile([P, E], BF16, name="qT", tag="qT", bufs=4)
+            qT = work.tile([P, E], BF16, name="qT", tag="qT")
             nc.vector.tensor_copy(out=qT[:], in_=st[("pq", gj)][:])
             st[("qT", gj)] = qT
 
         def scores(u):
             i, h = unit(u)
             qT = st[("qT", u // 4)]
-            np_ = passes(i)
-            mx = small.tile([P, 2], F32, name="mx", tag="mx")
             banks = []
-            for g in range(np_):
+            for g in range(passes(i)):
                 sg = ps_s.tile([P, 512], F32, name="sg", tag="s")
                 masked = (i < 8) and (g == i // 4)
                 nc.tensor.matmul(sg[:], lhsT=qT[:, h * P:(h + 1) * P], rhs=kT[:, g, h, :],
@@ -138,16 +129,21 @@ def tile_mha_t_kernel(tc, q, k, v, W_proj, out):
                 if masked:
                     nc.tensor.matmul(sg[:], lhsT=ident[:], rhs=maskb[:, i % 4, :], start=False, stop=True)
                 banks.append(sg)
-            for g in range(np_):
+            st[("s", u)] = banks
+
+        def maxs(u):
+            i, h = unit(u)
+            banks = st[("s", u)]
+            mx = small.tile([P, 2], F32, name="mx", tag="mx")
+            for g in range(passes(i)):
                 nc.vector.tensor_reduce(out=mx[:, g:g + 1], in_=live(banks[g][:], i, g), axis=AX.XY, op=ALU.max)
             nb = small.tile([P, 1], F32, name="nb", tag="nb")
-            if np_ == 2:
+            if passes(i) == 2:
                 nc.gpsimd.tensor_scalar(out=nb[:], in0=mx[:, 0:1], scalar1=mx[:, 1:2], scalar2=-SCALE,
                                         op0=ALU.max, op1=ALU.mult)
             else:
                 nc.gpsimd.tensor_scalar(out=nb[:], in0=mx[:, 0:1], scalar1=-SCALE, scalar2=0.0,
                                         op0=ALU.mult, op1=ALU.add)
-            st[("s", u)] = banks
             st[("nb", u)] = nb
 
         def exps(u):
@@ -167,9 +163,8 @@ def tile_mha_t_kernel(tc, q, k, v, W_proj, out):
 
         def e_transposes(u):
             i, h = unit(u)
-            e = st[("e", u)]
-            words = e[:].bitcast(F32)
-            pt = ps_t.tile([P, 4 * P], F32, name="pt", tag="x")
+            words = st[("e", u)][:].bitcast(F32)
+            pt = ps_t.tile([P, 4 * P], F32, name="pt", tag="t")
             for j in range(2 * passes(i)):
                 nc.tensor.transpose(pt[:, j * P:(j + 1) * P], words[:, j * P:(j + 1) * P], ident_w[:])
             st[("pt", u)] = pt
@@ -201,7 +196,7 @@ def tile_mha_t_kernel(tc, q, k, v, W_proj, out):
             np_ = passes(i)
             cod = st[("cod", gi)]
             sca = st[("sca", gi)]
-            o = ps_o.tile([P, E], F32, name="o", tag="x")
+            o = ps_g.tile([P, E], F32, name="o", tag="g")
             for h in range(H):
                 for g in range(np_):
                     nc.tensor.matmul_mx(
@@ -211,7 +206,7 @@ def tile_mha_t_kernel(tc, q, k, v, W_proj, out):
                         start=(g == 0), stop=(g == np_ - 1))
             st[("o", gi)] = o
 
-        def norm(gi):
+        def recip(gi):
             i = GROUP_ORDER[gi]
             rs = st[("rs", gi)]
             rinv = small.tile([P, H], F32, name="rinv", tag="rinv")
@@ -221,33 +216,36 @@ def tile_mha_t_kernel(tc, q, k, v, W_proj, out):
                 nc.vector.reciprocal(out=rinv[:], in_=rsum[:])
             else:
                 nc.vector.reciprocal(out=rinv[:], in_=rs[:, :, 0])
+            st[("rinv", gi)] = rinv
+
+        def norm(gi):
             ob = work.tile([P, H, D], BF16, name="ob", tag="ob")
             nc.vector.tensor_tensor(out=ob[:], in0=st[("o", gi)][:].rearrange("p (h d) -> p h d", h=H),
-                                    in1=rinv[:].unsqueeze(2).to_broadcast([P, H, D]), op=ALU.mult)
+                                    in1=st[("rinv", gi)][:].unsqueeze(2).to_broadcast([P, H, D]), op=ALU.mult)
             st[("ob", gi)] = ob
 
         def o_transposes(gi):
-            ob = st[("ob", gi)]
-            po = ps_m.tile([P, E], BF16, name="po", tag="x")
-            for t in range(4):
-                nc.tensor.transpose(po[:, t * P:(t + 1) * P], ob[:, t, :], ident[:])
+            words = st[("ob", gi)][:].rearrange("p h d -> p (h d)").bitcast(F32)
+            po = ps_g.tile([P, 2 * P], F32, name="po", tag="g")
+            for u in range(2):
+                nc.tensor.transpose(po[:, u * P:(u + 1) * P], words[:, u:2 * P:2], ident_w[:])
             st[("po", gi)] = po
 
         def o_copy(gi):
-            og = work.tile([P, P, 4], BF16, name="og", tag="og", align_bytes=64)
-            nc.any.tensor_copy(out=og[:], in_=st[("po", gi)][:].rearrange("p (t q) -> p q t", t=4))
+            og = work.tile([P, P, 2], F32, name="og", tag="og", align_bytes=64)
+            nc.scalar.copy(out=og[:], in_=st[("po", gi)][:].rearrange("p (u q) -> p q u", u=2))
             st[("og", gi)] = og
 
         def o_quant(gi):
             ocod = work.tile([P, P], U32, name="ocod", tag="ocod", align_bytes=64)
             osca = work.tile([P, P], U8, name="osca", tag="osca", align_bytes=64)
             nc.vector.quantize_mx(out=ocod[:].bitcast(FP8X4), scales=osca[:],
-                                  in_=st[("og", gi)][:].rearrange("p q t -> p (q t)"))
+                                  in_=st[("og", gi)][:].rearrange("p q u -> p (q u)").bitcast(BF16))
             st[("ocod", gi)] = ocod
             st[("osca", gi)] = osca
 
         def proj(gi):
-            y = ps_m.tile([P, E], F32, name="y", tag="x")
+            y = ps_g.tile([P, E], F32, name="y", tag="g")
             nc.tensor.matmul_mx(out=y[:], lhsT=st[("ocod", gi)][:].bitcast(FP8X4), lhsT_scale=st[("osca", gi)][:],
                                 rhs=wcod[:].bitcast(FP8X4), rhs_scale=wsca[:], start=True, stop=True)
             st[("y", gi)] = y
@@ -255,60 +253,90 @@ def tile_mha_t_kernel(tc, q, k, v, W_proj, out):
         def y_out(gi):
             i = GROUP_ORDER[gi]
             ysb = work.tile([P, E], F32, name="ysb", tag="ysb")
-            nc.any.tensor_copy(out=ysb[:], in_=st[("y", gi)][:])
+            nc.vector.tensor_copy(out=ysb[:], in_=st[("y", gi)][:])
             nc.sync.dma_start(out=out[i * P:(i + 1) * P, :], in_=ysb[:])
 
         def w_transposes(a):
-            pw = ps_m.tile([P, E], BF16, name="pw", tag="x")
-            for t in range(4):
-                nc.tensor.transpose(pw[:, t * P:(t + 1) * P], w_sb[:, a, t * P:(t + 1) * P], ident[:])
-            st[("pw", a)] = pw
+            words = w_sb[:, a, :].bitcast(F32)
+            pw = ps_g.tile([P, 2 * P], F32, name="pw", tag="g")
+            for u in range(2):
+                nc.tensor.transpose(pw[:, u * P:(u + 1) * P], words[:, u:2 * P:2], ident_w[:])
+            nc.scalar.copy(out=wg[:, a * P:(a + 1) * P, :], in_=pw[:].rearrange("p (u o) -> p o u", u=2))
 
-        def w_copy(a):
-            nc.vector.tensor_copy(out=wg[:, a * P:(a + 1) * P, :],
-                                  in_=st[("pw", a)][:].rearrange("p (t o) -> p o t", t=4))
+        def v_regroup(piece):
+            g, f0 = piece // 4, 128 * (piece % 4)
+            nc.gpsimd.tensor_scalar(out=vg[:, g, f0:f0 + 128, :], in0=v_sb[:, g, :, f0:f0 + 128].rearrange("p t f -> p f t"),
+                                    scalar1=1.0, scalar2=0.0, op0=ALU.mult, op1=ALU.add)
 
-        for s in range(-8, n_units + 12):
-            r = s % 4
-            if r == 1 and 0 <= (s + 7) // 4 < n_groups:
-                qt_copy((s + 7) // 4)
-            if r == 3 and 0 <= (s - 11) // 4 < n_groups:
-                y_out((s - 11) // 4)
-            if r == 0 and 0 <= (s - 8) // 4 < n_groups:
-                o_copy((s - 8) // 4)
-            if 1 <= s <= 4:
-                w_copy(s - 1)
+        def v_quant(g):
+            nc.vector.quantize_mx(out=vcod[:, g, :].bitcast(FP8X4), scales=vsca[:, g, :],
+                                  in_=vg[:, g].rearrange("p f t -> p (f t)"))
+
+        kt_transposes(0, 0)
+        qt_transposes(0)
+        qt_copy(0)
+        kt_transposes(1, 0)
+        kt_transposes(0, 1)
+        kt_transposes(1, 1)
+        scores(0)
+        maxs(0)
+        kt_transposes(0, 2)
+        kt_transposes(1, 2)
+        scores(1)
+        maxs(1)
+        kt_transposes(0, 3)
+        kt_transposes(1, 3)
+        qt_transposes(1)
+        qt_copy(1)
+
+        for s in range(-1, n_units + 12):
+            def at(offset):
+                return (s - offset) % 4 == 0 and 0 <= (s - offset) // 4 < n_groups
+
+            def group(offset):
+                return (s - offset) // 4
+
+            if 0 <= s < n_units:
+                exps(s)
+            if at(8):
+                o_copy(group(8))
             if 0 <= s - 1 < n_units:
                 e_copy(s - 1)
-            if 0 <= s + 2 < n_units:
-                scores(s + 2)
-            if 0 <= s + 1 < n_units:
-                exps(s + 1)
+            if 0 <= s + 3 < n_units:
+                scores(s + 3)
             if 0 <= s < n_units:
                 e_transposes(s)
-            if 0 <= s - 1 < n_units and (s - 1) % 2 == 1:
-                e_quant(s - 1)
-            if s == -1 or s == 0:
-                g = s + 1
-                nc.vector.tensor_copy(out=vg[:, g], in_=v_sb[:, g].rearrange("p t f -> p f t"))
-            if s == 1 or s == 2:
-                g = s - 1
-                nc.vector.quantize_mx(out=vcod[:, g, :].bitcast(FP8X4), scales=vsca[:, g, :],
-                                      in_=vg[:, g].rearrange("p f t -> p (f t)"))
-            if 0 <= s <= 3:
-                w_transposes(s)
-            if s == 6:
+            if at(6):
+                av(group(6))
+            if at(7):
+                o_transposes(group(7))
+            if at(-8) and group(-8) > 1:
+                qt_transposes(group(-8))
+            if at(9):
+                proj(group(9))
+            if s in (1, 2, 3, 5):
+                w_transposes((1, 2, 3, 5).index(s))
+            if 0 <= s + 3 < n_units:
+                maxs(s + 3)
+            if 0 <= s - 2 < n_units and s % 2 == 1:
+                e_quant(s - 2)
+            if at(8):
+                o_quant(group(8))
+            if at(5):
+                recip(group(5))
+            if at(6):
+                norm(group(6))
+            if at(-8) and group(-8) > 1:
+                qt_copy(group(-8))
+            if at(9):
+                y_out(group(9))
+            if 0 <= s < 4:
+                v_regroup(2 * s)
+                v_regroup(2 * s + 1)
+            if s == 4 or s == 5:
+                v_quant(s - 4)
+            if s == 7:
                 nc.vector.quantize_mx(out=wcod[:].bitcast(FP8X4), scales=wsca[:],
-                                      in_=wg[:].rearrange("p o t -> p (o t)"))
-            if r == 0 and 0 <= (s - 8) // 4 < n_groups:
-                o_quant((s - 8) // 4)
-            if r == 1 and 0 <= (s - 5) // 4 < n_groups:
-                av((s - 5) // 4)
-            if r == 1 and 0 <= (s - 9) // 4 < n_groups:
-                proj((s - 9) // 4)
-            if r == 2 and 0 <= (s - 6) // 4 < n_groups:
-                norm((s - 6) // 4)
-            if r == 3 and 0 <= (s - 7) // 4 < n_groups:
-                o_transposes((s - 7) // 4)
-            if r == 0 and 0 <= (s + 8) // 4 < n_groups:
-                qt_transposes((s + 8) // 4)
+                                      in_=wg[:].rearrange("p o u -> p (o u)").bitcast(BF16))
+            if 8 <= s < 12:
+                mask_select(s - 8)

@@ -75,10 +75,11 @@ def tile_mha_t_kernel(tc, q, k, v, W_proj, out):
         st = {}
 
         def mask_select(j):
-            sel = maskb[:, j, :].rearrange("p (u c e) -> p u c e", u=2, e=2)
-            nc.gpsimd.affine_select(
-                out=sel, in_=sel, pattern=[[-2, 2], [-4, P], [-1, 2]],
-                compare_op=ALU.is_ge, fill=MASK_FILL, base=128 * j, channel_multiplier=1)
+            for e in range(2):
+                sel = maskb[:, j, :].rearrange("p (u c e) -> p u c e", u=2, e=2)[:, :, :, e]
+                nc.gpsimd.affine_select(
+                    out=sel, in_=sel, pattern=[[-2, 2], [-4, P]],
+                    compare_op=ALU.is_ge, fill=MASK_FILL, base=128 * j - e, channel_multiplier=1)
 
         def kt_transposes(g, h):
             pk = ps_s.tile([P, 512], BF16, name="pk", tag="s")
@@ -206,16 +207,18 @@ def tile_mha_t_kernel(tc, q, k, v, W_proj, out):
                         start=(g == 0), stop=(g == np_ - 1))
             st[("o", gi)] = o
 
-        def recip(gi):
-            i = GROUP_ORDER[gi]
+        def row_sums(gi):
             rs = st[("rs", gi)]
-            rinv = small.tile([P, H], F32, name="rinv", tag="rinv")
-            if passes(i) == 2:
+            if passes(GROUP_ORDER[gi]) == 2:
                 rsum = small.tile([P, H], F32, name="rsum", tag="rsum")
                 nc.gpsimd.tensor_tensor(out=rsum[:], in0=rs[:, :, 0], in1=rs[:, :, 1], op=ALU.add)
-                nc.vector.reciprocal(out=rinv[:], in_=rsum[:])
+                st[("rsum", gi)] = rsum[:]
             else:
-                nc.vector.reciprocal(out=rinv[:], in_=rs[:, :, 0])
+                st[("rsum", gi)] = rs[:, :, 0]
+
+        def recip(gi):
+            rinv = small.tile([P, H], F32, name="rinv", tag="rinv")
+            nc.vector.reciprocal(out=rinv[:], in_=st[("rsum", gi)])
             st[("rinv", gi)] = rinv
 
         def norm(gi):
@@ -298,10 +301,14 @@ def tile_mha_t_kernel(tc, q, k, v, W_proj, out):
 
             if 0 <= s < n_units:
                 exps(s)
-            if at(8):
-                o_copy(group(8))
             if 0 <= s - 1 < n_units:
                 e_copy(s - 1)
+            if at(8):
+                o_copy(group(8))
+            if at(5):
+                row_sums(group(5))
+            if at(6):
+                recip(group(6))
             if 0 <= s + 3 < n_units:
                 scores(s + 3)
             if 0 <= s < n_units:
@@ -318,18 +325,16 @@ def tile_mha_t_kernel(tc, q, k, v, W_proj, out):
                 w_transposes((1, 2, 3, 5).index(s))
             if 0 <= s + 3 < n_units:
                 maxs(s + 3)
-            if 0 <= s - 2 < n_units and s % 2 == 1:
-                e_quant(s - 2)
-            if at(8):
-                o_quant(group(8))
-            if at(5):
-                recip(group(5))
             if at(6):
                 norm(group(6))
             if at(-8) and group(-8) > 1:
                 qt_copy(group(-8))
             if at(9):
                 y_out(group(9))
+            if at(8):
+                o_quant(group(8))
+            if 0 <= s - 2 < n_units and s % 2 == 1:
+                e_quant(s - 2)
             if 0 <= s < 4:
                 v_regroup(2 * s)
                 v_regroup(2 * s + 1)

@@ -29,9 +29,7 @@ def tile_mha_t_kernel(tc, q, k, v, W_proj, out):
         const = ctx.enter_context(tc.tile_pool(name="const", bufs=1))
         work = ctx.enter_context(tc.tile_pool(name="work", bufs=4))
         small = ctx.enter_context(tc.tile_pool(name="small", bufs=6))
-        ps_s = ctx.enter_context(tc.psum_pool(name="ps_s", bufs=6))
-        ps_t = ctx.enter_context(tc.psum_pool(name="ps_t", bufs=1))
-        ps_g = ctx.enter_context(tc.psum_pool(name="ps_g", bufs=1))
+        psum = ctx.enter_context(tc.psum_pool(name="psum", bufs=8))
 
         k_sb = const.tile([P, 2, 4, E], BF16, name="k_sb")
         v_sb = const.tile([P, 2, 4, E], BF16, name="v_sb")
@@ -53,8 +51,12 @@ def tile_mha_t_kernel(tc, q, k, v, W_proj, out):
         make_identity(nc, ident[:])
         ident_w = const.tile([P, P], F32, name="ident_w")
         make_identity(nc, ident_w[:])
-        maskb = const.tile([P, 4, 4 * P], BF16, name="maskb")
+        maskb = const.tile([P, 2, 32, 2], BF16, name="maskb")
         nc.gpsimd.memset(maskb[:], 0.0)
+        for e in range(2):
+            nc.gpsimd.affine_select(
+                out=maskb[:, :, :, e], in_=maskb[:, :, :, e], pattern=[[-2, 2], [-4, 32]],
+                compare_op=ALU.is_ge, fill=MASK_FILL, base=-e, channel_multiplier=1)
 
         kT = const.tile([P, 2, H, 512], BF16, name="kT")
         vg = const.tile([P, 2, E, 4], BF16, name="vg", align_bytes=64)
@@ -74,20 +76,13 @@ def tile_mha_t_kernel(tc, q, k, v, W_proj, out):
         n_units = 4 * n_groups
         st = {}
 
-        def mask_select(j):
-            for e in range(2):
-                sel = maskb[:, j, :].rearrange("p (u c e) -> p u c e", u=2, e=2)[:, :, :, e]
-                nc.gpsimd.affine_select(
-                    out=sel, in_=sel, pattern=[[-2, 2], [-4, P]],
-                    compare_op=ALU.is_ge, fill=MASK_FILL, base=128 * j - e, channel_multiplier=1)
-
         def kt_transposes(g, h):
-            pk = ps_s.tile([P, 512], BF16, name="pk", tag="s")
+            pk = psum.tile([P, 512], BF16, name="pk", tag="x")
             for t in range(4):
                 nc.tensor.transpose(pk[:, t * P:(t + 1) * P], k_sb[:, g, t, h * D:(h + 1) * D], ident[:])
             dst = kT[:, g, h, :].rearrange("p (u c e) -> p u c e", u=2, e=2)
             src = pk[:].rearrange("p (u e c) -> p u c e", u=2, e=2)
-            if g == 0:
+            if g == 0 and h == 0:
                 nc.vector.tensor_copy(out=dst, in_=src)
             else:
                 nc.scalar.copy(out=dst, in_=src)
@@ -108,7 +103,7 @@ def tile_mha_t_kernel(tc, q, k, v, W_proj, out):
 
         def qt_transposes(gj):
             i = GROUP_ORDER[gj]
-            pq = ps_g.tile([P, E], BF16, name="pq", tag="g")
+            pq = psum.tile([P, E], BF16, name="pq", tag="x")
             for h in range(H):
                 nc.tensor.transpose(pq[:, h * P:(h + 1) * P], q_sb[:, i, h * D:(h + 1) * D], ident[:])
             st[("pq", gj)] = pq
@@ -123,12 +118,14 @@ def tile_mha_t_kernel(tc, q, k, v, W_proj, out):
             qT = st[("qT", u // 4)]
             banks = []
             for g in range(passes(i)):
-                sg = ps_s.tile([P, 512], F32, name="sg", tag="s")
+                sg = psum.tile([P, 512], F32, name="sg", tag="x")
                 masked = (i < 8) and (g == i // 4)
-                nc.tensor.matmul(sg[:], lhsT=qT[:, h * P:(h + 1) * P], rhs=kT[:, g, h, :],
+                nc.tensor.matmul(live(sg[:], i, g), lhsT=qT[:, h * P:(h + 1) * P], rhs=live(kT[:, g, h, :], i, g),
                                  start=True, stop=not masked)
                 if masked:
-                    nc.tensor.matmul(sg[:], lhsT=ident[:], rhs=maskb[:, i % 4, :], start=False, stop=True)
+                    j = i % 4
+                    nc.tensor.matmul(sg[:].rearrange("p (u w) -> p u w", u=2)[:, :, 64 * j:64 * j + 64], lhsT=ident[:],
+                                     rhs=maskb[:].rearrange("p u c e -> p u (c e)"), start=False, stop=True)
                 banks.append(sg)
             st[("s", u)] = banks
 
@@ -165,7 +162,7 @@ def tile_mha_t_kernel(tc, q, k, v, W_proj, out):
         def e_transposes(u):
             i, h = unit(u)
             words = st[("e", u)][:].bitcast(F32)
-            pt = ps_t.tile([P, 4 * P], F32, name="pt", tag="t")
+            pt = psum.tile([P, 4 * P], F32, name="pt", tag="x")
             for j in range(2 * passes(i)):
                 nc.tensor.transpose(pt[:, j * P:(j + 1) * P], words[:, j * P:(j + 1) * P], ident_w[:])
             st[("pt", u)] = pt
@@ -197,7 +194,7 @@ def tile_mha_t_kernel(tc, q, k, v, W_proj, out):
             np_ = passes(i)
             cod = st[("cod", gi)]
             sca = st[("sca", gi)]
-            o = ps_g.tile([P, E], F32, name="o", tag="g")
+            o = psum.tile([P, E], F32, name="o", tag="x")
             for h in range(H):
                 for g in range(np_):
                     nc.tensor.matmul_mx(
@@ -229,7 +226,7 @@ def tile_mha_t_kernel(tc, q, k, v, W_proj, out):
 
         def o_transposes(gi):
             words = st[("ob", gi)][:].rearrange("p h d -> p (h d)").bitcast(F32)
-            po = ps_g.tile([P, 2 * P], F32, name="po", tag="g")
+            po = psum.tile([P, 2 * P], F32, name="po", tag="x")
             for u in range(2):
                 nc.tensor.transpose(po[:, u * P:(u + 1) * P], words[:, u:2 * P:2], ident_w[:])
             st[("po", gi)] = po
@@ -248,7 +245,7 @@ def tile_mha_t_kernel(tc, q, k, v, W_proj, out):
             st[("osca", gi)] = osca
 
         def proj(gi):
-            y = ps_g.tile([P, E], F32, name="y", tag="g")
+            y = psum.tile([P, E], F32, name="y", tag="x")
             nc.tensor.matmul_mx(out=y[:], lhsT=st[("ocod", gi)][:].bitcast(FP8X4), lhsT_scale=st[("osca", gi)][:],
                                 rhs=wcod[:].bitcast(FP8X4), rhs_scale=wsca[:], start=True, stop=True)
             st[("y", gi)] = y
@@ -261,7 +258,7 @@ def tile_mha_t_kernel(tc, q, k, v, W_proj, out):
 
         def w_transposes(a):
             words = w_sb[:, a, :].bitcast(F32)
-            pw = ps_g.tile([P, 2 * P], F32, name="pw", tag="g")
+            pw = psum.tile([P, 2 * P], F32, name="pw", tag="x")
             for u in range(2):
                 nc.tensor.transpose(pw[:, u * P:(u + 1) * P], words[:, u:2 * P:2], ident_w[:])
             nc.scalar.copy(out=wg[:, a * P:(a + 1) * P, :], in_=pw[:].rearrange("p (u o) -> p o u", u=2))
@@ -287,8 +284,6 @@ def tile_mha_t_kernel(tc, q, k, v, W_proj, out):
         kt_transposes(1, 2)
         scores(1)
         maxs(1)
-        kt_transposes(0, 3)
-        kt_transposes(1, 3)
         qt_transposes(1)
         qt_copy(1)
 
@@ -301,6 +296,9 @@ def tile_mha_t_kernel(tc, q, k, v, W_proj, out):
 
             if 0 <= s < n_units:
                 exps(s)
+            if s == 0:
+                kt_transposes(0, 3)
+                kt_transposes(1, 3)
             if 0 <= s - 1 < n_units:
                 e_copy(s - 1)
             if at(8):
@@ -325,6 +323,8 @@ def tile_mha_t_kernel(tc, q, k, v, W_proj, out):
                 w_transposes((1, 2, 3, 5).index(s))
             if 0 <= s + 3 < n_units:
                 maxs(s + 3)
+            if 0 <= s - 1 < n_units and s % 2 == 0:
+                e_quant(s - 1)
             if at(6):
                 norm(group(6))
             if at(-8) and group(-8) > 1:
@@ -333,8 +333,6 @@ def tile_mha_t_kernel(tc, q, k, v, W_proj, out):
                 y_out(group(9))
             if at(8):
                 o_quant(group(8))
-            if 0 <= s - 2 < n_units and s % 2 == 1:
-                e_quant(s - 2)
             if 0 <= s < 4:
                 v_regroup(2 * s)
                 v_regroup(2 * s + 1)
@@ -343,5 +341,3 @@ def tile_mha_t_kernel(tc, q, k, v, W_proj, out):
             if s == 7:
                 nc.vector.quantize_mx(out=wcod[:].bitcast(FP8X4), scales=wsca[:],
                                       in_=wg[:].rearrange("p o u -> p (o u)").bitcast(BF16))
-            if 8 <= s < 12:
-                mask_select(s - 8)

@@ -113,11 +113,15 @@ def tile_mha_t_kernel(tc, q, k, v, W_proj, out):
             nc.vector.tensor_copy(out=qT[:], in_=st[("pq", gj)][:])
             st[("qT", gj)] = qT
 
-        def scores(u):
+        def scores(u, gs):
+            if not 0 <= u < n_units:
+                return
             i, h = unit(u)
             qT = st[("qT", u // 4)]
-            banks = []
-            for g in range(passes(i)):
+            banks = st.setdefault(("s", u), {})
+            for g in gs:
+                if g >= passes(i):
+                    continue
                 sg = psum.tile([P, 512], F32, name="sg", tag="x")
                 masked = (i < 8) and (g == i // 4)
                 nc.tensor.matmul(live(sg[:], i, g), lhsT=qT[:, h * P:(h + 1) * P], rhs=live(kT[:, g, h, :], i, g),
@@ -126,8 +130,7 @@ def tile_mha_t_kernel(tc, q, k, v, W_proj, out):
                     j = i % 4
                     nc.tensor.matmul(sg[:].rearrange("p (u w) -> p u w", u=2)[:, :, 64 * j:64 * j + 64], lhsT=ident[:],
                                      rhs=maskb[:].rearrange("p u c e -> p u (c e)"), start=False, stop=True)
-                banks.append(sg)
-            st[("s", u)] = banks
+                banks[g] = sg
 
         def maxs(u):
             i, h = unit(u)
@@ -233,7 +236,11 @@ def tile_mha_t_kernel(tc, q, k, v, W_proj, out):
 
         def o_copy(gi):
             og = work.tile([P, P, 2], F32, name="og", tag="og", align_bytes=64)
-            nc.scalar.copy(out=og[:], in_=st[("po", gi)][:].rearrange("p (u q) -> p q u", u=2))
+            src = st[("po", gi)][:].rearrange("p (u q) -> p q u", u=2)
+            if gi % 2 == 0:
+                nc.scalar.copy(out=og[:], in_=src)
+            else:
+                nc.vector.tensor_copy(out=og[:], in_=src)
             st[("og", gi)] = og
 
         def o_quant(gi):
@@ -252,7 +259,7 @@ def tile_mha_t_kernel(tc, q, k, v, W_proj, out):
 
         def y_out(gi):
             i = GROUP_ORDER[gi]
-            ysb = work.tile([P, E], F32, name="ysb", tag="ysb")
+            ysb = work.tile([P, E], F32, name="ysb", tag="ysb", bufs=32)
             nc.vector.tensor_copy(out=ysb[:], in_=st[("y", gi)][:])
             nc.sync.dma_start(out=out[i * P:(i + 1) * P, :], in_=ysb[:])
 
@@ -278,16 +285,8 @@ def tile_mha_t_kernel(tc, q, k, v, W_proj, out):
         kt_transposes(1, 0)
         kt_transposes(0, 1)
         kt_transposes(1, 1)
-        scores(0)
-        maxs(0)
-        kt_transposes(0, 2)
-        kt_transposes(1, 2)
-        scores(1)
-        maxs(1)
-        qt_transposes(1)
-        qt_copy(1)
 
-        for s in range(-1, n_units + 12):
+        for s in range(-2, n_units + 18):
             def at(offset):
                 return (s - offset) % 4 == 0 and 0 <= (s - offset) // 4 < n_groups
 
@@ -296,48 +295,55 @@ def tile_mha_t_kernel(tc, q, k, v, W_proj, out):
 
             if 0 <= s < n_units:
                 exps(s)
-            if s == 0:
-                kt_transposes(0, 3)
-                kt_transposes(1, 3)
+            scores(s + 2, (1,))
+            if 0 <= s - 1 < n_units:
+                e_transposes(s - 1)
+            scores(s + 2, (0,))
             if 0 <= s - 1 < n_units:
                 e_copy(s - 1)
-            if at(8):
-                o_copy(group(8))
+            if at(10) and group(10) % 2 == 0:
+                o_copy(group(10))
             if at(5):
                 row_sums(group(5))
-            if at(6):
-                recip(group(6))
-            if 0 <= s + 3 < n_units:
-                scores(s + 3)
-            if 0 <= s < n_units:
-                e_transposes(s)
-            if at(6):
-                av(group(6))
+            if s % 2 == 0 and 0 <= s - 3 < n_units:
+                e_quant(s - 3)
             if at(7):
-                o_transposes(group(7))
-            if at(-8) and group(-8) > 1:
-                qt_transposes(group(-8))
-            if at(9):
-                proj(group(9))
-            if s in (1, 2, 3, 5):
-                w_transposes((1, 2, 3, 5).index(s))
-            if 0 <= s + 3 < n_units:
-                maxs(s + 3)
-            if 0 <= s - 1 < n_units and s % 2 == 0:
-                e_quant(s - 1)
-            if at(6):
-                norm(group(6))
-            if at(-8) and group(-8) > 1:
-                qt_copy(group(-8))
-            if at(9):
-                y_out(group(9))
+                recip(group(7))
             if at(8):
-                o_quant(group(8))
+                norm(group(8))
+            if at(17):
+                y_out(group(17))
+            if at(-5) and group(-5) > 1:
+                qt_copy(group(-5))
+            if at(10) and group(10) % 2 == 1:
+                o_copy(group(10))
+            if at(15):
+                proj(group(15))
+            if at(8):
+                o_transposes(group(8))
+            if at(7):
+                av(group(7))
+            if at(-7) and group(-7) > 1:
+                qt_transposes(group(-7))
+            if s in (2, 3, 6, 10):
+                w_transposes((2, 3, 6, 10).index(s))
+            if 0 <= s + 2 < n_units:
+                maxs(s + 2)
+            if at(12):
+                o_quant(group(12))
+            if s == -2:
+                kt_transposes(0, 2)
+                kt_transposes(1, 2)
+            if s == -1:
+                qt_transposes(1)
+                qt_copy(1)
+                kt_transposes(0, 3)
+                kt_transposes(1, 3)
             if 0 <= s < 4:
                 v_regroup(2 * s)
                 v_regroup(2 * s + 1)
             if s == 4 or s == 5:
                 v_quant(s - 4)
-            if s == 7:
+            if s == 12:
                 nc.vector.quantize_mx(out=wcod[:].bitcast(FP8X4), scales=wsca[:],
                                       in_=wg[:].rearrange("p o u -> p (o u)").bitcast(BF16))

@@ -132,12 +132,20 @@ def tile_mha_t_kernel(tc, q, k, v, W_proj, out):
                                      rhs=maskb[:].rearrange("p u c e -> p u (c e)"), start=False, stop=True)
                 banks[g] = sg
 
-        def maxs(u):
+        def maxs(u, g):
+            if not 0 <= u < n_units or g >= passes(unit(u)[0]):
+                return
             i, h = unit(u)
-            banks = st[("s", u)]
-            mx = small.tile([P, 2], F32, name="mx", tag="mx")
-            for g in range(passes(i)):
-                nc.vector.tensor_reduce(out=mx[:, g:g + 1], in_=live(banks[g][:], i, g), axis=AX.XY, op=ALU.max)
+            if g == 0:
+                st[("mx", u)] = small.tile([P, 2], F32, name="mx", tag="mx")
+            mx = st[("mx", u)]
+            nc.vector.tensor_reduce(out=mx[:, g:g + 1], in_=live(st[("s", u)][g][:], i, g), axis=AX.XY, op=ALU.max)
+
+        def neg_max(u):
+            if not 0 <= u < n_units:
+                return
+            i, h = unit(u)
+            mx = st[("mx", u)]
             nb = small.tile([P, 1], F32, name="nb", tag="nb")
             if passes(i) == 2:
                 nc.gpsimd.tensor_scalar(out=nb[:], in0=mx[:, 0:1], scalar1=mx[:, 1:2], scalar2=-SCALE,
@@ -236,11 +244,7 @@ def tile_mha_t_kernel(tc, q, k, v, W_proj, out):
 
         def o_copy(gi):
             og = work.tile([P, P, 2], F32, name="og", tag="og", align_bytes=64)
-            src = st[("po", gi)][:].rearrange("p (u q) -> p q u", u=2)
-            if gi % 2 == 0:
-                nc.scalar.copy(out=og[:], in_=src)
-            else:
-                nc.vector.tensor_copy(out=og[:], in_=src)
+            nc.scalar.copy(out=og[:], in_=st[("po", gi)][:].rearrange("p (u q) -> p q u", u=2))
             st[("og", gi)] = og
 
         def o_quant(gi):
@@ -283,10 +287,8 @@ def tile_mha_t_kernel(tc, q, k, v, W_proj, out):
         qt_transposes(0)
         qt_copy(0)
         kt_transposes(1, 0)
-        kt_transposes(0, 1)
-        kt_transposes(1, 1)
 
-        for s in range(-2, n_units + 18):
+        for s in range(-3, n_units + 15):
             def at(offset):
                 return (s - offset) % 4 == 0 and 0 <= (s - offset) // 4 < n_groups
 
@@ -295,55 +297,49 @@ def tile_mha_t_kernel(tc, q, k, v, W_proj, out):
 
             if 0 <= s < n_units:
                 exps(s)
-            scores(s + 2, (1,))
+            if at(14):
+                proj(group(14))
+            if at(-5) and group(-5) > 0:
+                qt_transposes(group(-5))
+            if at(10):
+                o_transposes(group(10))
+            if s in (1, 4, 5, 8):
+                w_transposes((1, 4, 5, 8).index(s))
             if 0 <= s - 1 < n_units:
                 e_transposes(s - 1)
-            scores(s + 2, (0,))
-            if 0 <= s - 1 < n_units:
-                e_copy(s - 1)
-            if at(10) and group(10) % 2 == 0:
-                o_copy(group(10))
-            if at(5):
-                row_sums(group(5))
-            if s % 2 == 0 and 0 <= s - 3 < n_units:
-                e_quant(s - 3)
-            if at(7):
-                recip(group(7))
-            if at(8):
-                norm(group(8))
-            if at(17):
-                y_out(group(17))
-            if at(-5) and group(-5) > 1:
-                qt_copy(group(-5))
-            if at(10) and group(10) % 2 == 1:
-                o_copy(group(10))
-            if at(15):
-                proj(group(15))
-            if at(8):
-                o_transposes(group(8))
+            scores(s + 2, (1,))
+            scores(s + 3, (0,))
             if at(7):
                 av(group(7))
-            if at(-7) and group(-7) > 1:
-                qt_transposes(group(-7))
-            if s in (2, 3, 6, 10):
-                w_transposes((2, 3, 6, 10).index(s))
-            if 0 <= s + 2 < n_units:
-                maxs(s + 2)
+            if at(10):
+                o_copy(group(10))
+            if 0 <= s - 1 < n_units:
+                e_copy(s - 1)
+            if at(14):
+                y_out(group(14))
+            if at(9):
+                norm(group(9))
+            maxs(s + 2, 0)
+            if at(7):
+                recip(group(7))
+            if s % 2 == 0 and 0 <= s - 3 < n_units:
+                e_quant(s - 3)
+            if s == 3 or s == 5:
+                v_quant((s - 3) // 2)
+            if s == 11:
+                nc.vector.quantize_mx(out=wcod[:].bitcast(FP8X4), scales=wsca[:],
+                                      in_=wg[:].rearrange("p o u -> p (o u)").bitcast(BF16))
+            if at(-5) and group(-5) > 0:
+                qt_copy(group(-5))
             if at(12):
                 o_quant(group(12))
-            if s == -2:
-                kt_transposes(0, 2)
-                kt_transposes(1, 2)
-            if s == -1:
-                qt_transposes(1)
-                qt_copy(1)
-                kt_transposes(0, 3)
-                kt_transposes(1, 3)
+            maxs(s + 2, 1)
+            if at(5):
+                row_sums(group(5))
+            neg_max(s + 2)
             if 0 <= s < 4:
                 v_regroup(2 * s)
                 v_regroup(2 * s + 1)
-            if s == 4 or s == 5:
-                v_quant(s - 4)
-            if s == 12:
-                nc.vector.quantize_mx(out=wcod[:].bitcast(FP8X4), scales=wsca[:],
-                                      in_=wg[:].rearrange("p o u -> p (o u)").bitcast(BF16))
+            if s < 0:
+                kt_transposes(0, s + 4)
+                kt_transposes(1, s + 4)

@@ -20,7 +20,7 @@ AX = mybir.AxisListType
 P = 128
 SCALE = 1.0 / math.sqrt(D)
 MASK_FILL = -131072.0
-GROUP_ORDER = list(range(8, 32)) + list(range(4, 8)) + list(range(0, 4))
+GROUP_ORDER = list(range(0, 4)) + list(range(8, 32)) + list(range(7, 3, -1))
 
 
 def tile_mha_t_kernel(tc, q, k, v, W_proj, out):
@@ -37,12 +37,12 @@ def tile_mha_t_kernel(tc, q, k, v, W_proj, out):
         q_sb = const.tile([P, 32, E], BF16, name="q_sb")
         q_view = q.rearrange("(i p) h d -> p i (h d)", p=P)
         k_view = k.rearrange("(g c t) h d -> c g t (h d)", g=2, t=4)
-        chunk_order = [2, 3, 4, 5, 6, 7, 1, 0]
+        chunk_order = [0, 2, 3, 4, 5, 6, 7, 1]
         nc.sync.dma_start(out=k_sb[:, 0], in_=k_view[:, 0])
-        nc.sync.dma_start(out=q_sb[:, 8:9, :], in_=q_view[:, 8:9, :])
-        nc.sync.dma_start(out=k_sb[:, 1], in_=k_view[:, 1])
-        nc.sync.dma_start(out=q_sb[:, 9:12, :], in_=q_view[:, 9:12, :])
+        nc.sync.dma_start(out=q_sb[:, 0:1, :], in_=q_view[:, 0:1, :])
+        nc.sync.dma_start(out=q_sb[:, 1:4, :], in_=q_view[:, 1:4, :])
         nc.sync.dma_start(out=v_sb[:], in_=v.rearrange("(g c t) h d -> c g t (h d)", g=2, t=4))
+        nc.sync.dma_start(out=k_sb[:, 1], in_=k_view[:, 1])
         nc.sync.dma_start(out=w_sb[:], in_=W_proj.rearrange("(a p) f -> p a f", p=P))
         for a in chunk_order[1:]:
             nc.sync.dma_start(out=q_sb[:, 4 * a:4 * a + 4, :], in_=q_view[:, 4 * a:4 * a + 4, :])
@@ -274,8 +274,8 @@ def tile_mha_t_kernel(tc, q, k, v, W_proj, out):
                 nc.tensor.transpose(pw[:, u * P:(u + 1) * P], words[:, u:2 * P:2], ident_w[:])
             nc.scalar.copy(out=wg[:, a * P:(a + 1) * P, :], in_=pw[:].rearrange("p (u o) -> p o u", u=2))
 
-        def v_regroup(piece):
-            g, f0 = piece // 4, 128 * (piece % 4)
+        def v_regroup(g, piece):
+            f0 = 128 * piece
             nc.gpsimd.tensor_scalar(out=vg[:, g, f0:f0 + 128, :], in0=v_sb[:, g, :, f0:f0 + 128].rearrange("p t f -> p f t"),
                                     scalar1=1.0, scalar2=0.0, op0=ALU.mult, op1=ALU.add)
 
@@ -286,7 +286,8 @@ def tile_mha_t_kernel(tc, q, k, v, W_proj, out):
         kt_transposes(0, 0)
         qt_transposes(0)
         qt_copy(0)
-        kt_transposes(1, 0)
+        kt_transposes(0, 1)
+        kt_transposes(0, 2)
 
         for s in range(-3, n_units + 15):
             def at(offset):
@@ -297,6 +298,10 @@ def tile_mha_t_kernel(tc, q, k, v, W_proj, out):
 
             if 0 <= s < n_units:
                 exps(s)
+            if s == -2:
+                kt_transposes(0, 3)
+            if 13 <= s < 17:
+                kt_transposes(1, s - 13)
             if at(14):
                 proj(group(14))
             if at(-5) and group(-5) > 0:
@@ -324,8 +329,10 @@ def tile_mha_t_kernel(tc, q, k, v, W_proj, out):
                 recip(group(7))
             if s % 2 == 0 and 0 <= s - 3 < n_units:
                 e_quant(s - 3)
-            if s == 3 or s == 5:
-                v_quant((s - 3) // 2)
+            if s == 5:
+                v_quant(0)
+            if s == 15:
+                v_quant(1)
             if s == 11:
                 nc.vector.quantize_mx(out=wcod[:].bitcast(FP8X4), scales=wsca[:],
                                       in_=wg[:].rearrange("p o u -> p (o u)").bitcast(BF16))
@@ -338,8 +345,6 @@ def tile_mha_t_kernel(tc, q, k, v, W_proj, out):
                 row_sums(group(5))
             neg_max(s + 2)
             if 0 <= s < 4:
-                v_regroup(2 * s)
-                v_regroup(2 * s + 1)
-            if s < 0:
-                kt_transposes(0, s + 4)
-                kt_transposes(1, s + 4)
+                v_regroup(0, s)
+            if 8 <= s < 12:
+                v_regroup(1, s - 8)

@@ -36,13 +36,17 @@ def tile_mha_t_kernel(tc, q, k, v, W_proj, out):
         w_sb = const.tile([P, 4, E], BF16, name="w_sb")
         q_sb = const.tile([P, 32, E], BF16, name="q_sb")
         q_view = q.rearrange("(i p) h d -> p i (h d)", p=P)
-        k_view = k.rearrange("(g c t) h d -> c g t (h d)", g=2, t=4)
+        k_view = k.rearrange("(g a c u e) h d -> g e u c a (h d)", g=2, a=2, u=2, e=2)
         chunk_order = [0, 2, 3, 4, 5, 6, 7, 1]
-        nc.sync.dma_start(out=k_sb[:, 0], in_=k_view[:, 0])
+        for u in range(2):
+            for e in range(2):
+                nc.sync.dma_start(out=k_sb[e:P:2, 0, 2 * u:2 * u + 2, :], in_=k_view[0, e, u])
         nc.sync.dma_start(out=q_sb[:, 0:1, :], in_=q_view[:, 0:1, :])
         nc.sync.dma_start(out=q_sb[:, 1:4, :], in_=q_view[:, 1:4, :])
         nc.sync.dma_start(out=v_sb[:], in_=v.rearrange("(g c t) h d -> c g t (h d)", g=2, t=4))
-        nc.sync.dma_start(out=k_sb[:, 1], in_=k_view[:, 1])
+        for u in range(2):
+            for e in range(2):
+                nc.sync.dma_start(out=k_sb[e:P:2, 1, 2 * u:2 * u + 2, :], in_=k_view[1, e, u])
         nc.sync.dma_start(out=w_sb[:], in_=W_proj.rearrange("(a p) f -> p a f", p=P))
         for a in chunk_order[1:]:
             nc.sync.dma_start(out=q_sb[:, 4 * a:4 * a + 4, :], in_=q_view[:, 4 * a:4 * a + 4, :])
@@ -80,12 +84,10 @@ def tile_mha_t_kernel(tc, q, k, v, W_proj, out):
             pk = psum.tile([P, 512], BF16, name="pk", tag="x")
             for t in range(4):
                 nc.tensor.transpose(pk[:, t * P:(t + 1) * P], k_sb[:, g, t, h * D:(h + 1) * D], ident[:])
-            dst = kT[:, g, h, :].rearrange("p (u c e) -> p u c e", u=2, e=2)
-            src = pk[:].rearrange("p (u e c) -> p u c e", u=2, e=2)
-            if g == 0 and h == 0:
-                nc.vector.tensor_copy(out=dst, in_=src)
+            if (g, h) in ((0, 0), (1, 1), (1, 3)):
+                nc.vector.tensor_copy(out=kT[:, g, h, :], in_=pk[:])
             else:
-                nc.scalar.copy(out=dst, in_=src)
+                nc.scalar.copy(out=kT[:, g, h, :], in_=pk[:])
 
         def passes(i):
             return 1 if i < 4 else 2
@@ -308,18 +310,18 @@ def tile_mha_t_kernel(tc, q, k, v, W_proj, out):
                 qt_transposes(group(-5))
             if at(10):
                 o_transposes(group(10))
-            if s in (1, 4, 5, 8):
-                w_transposes((1, 4, 5, 8).index(s))
+            if s in (5, 8, 9, 12):
+                w_transposes((5, 8, 9, 12).index(s))
             if 0 <= s - 1 < n_units:
                 e_transposes(s - 1)
-            scores(s + 2, (1,))
             scores(s + 3, (0,))
+            scores(s + 2, (1,))
             if at(7):
                 av(group(7))
-            if at(10):
-                o_copy(group(10))
             if 0 <= s - 1 < n_units:
                 e_copy(s - 1)
+            if at(10):
+                o_copy(group(10))
             if at(14):
                 y_out(group(14))
             if at(9):
@@ -333,7 +335,7 @@ def tile_mha_t_kernel(tc, q, k, v, W_proj, out):
                 v_quant(0)
             if s == 15:
                 v_quant(1)
-            if s == 11:
+            if s == 13:
                 nc.vector.quantize_mx(out=wcod[:].bitcast(FP8X4), scales=wsca[:],
                                       in_=wg[:].rearrange("p o u -> p (o u)").bitcast(BF16))
             if at(-5) and group(-5) > 0:

@@ -43,12 +43,15 @@ def tile_mha_t_kernel(tc, q, k, v, W_proj, out):
                 nc.sync.dma_start(out=k_sb[e:P:2, 0, 2 * u:2 * u + 2, :], in_=k_view[0, e, u])
         nc.sync.dma_start(out=q_sb[:, 0:1, :], in_=q_view[:, 0:1, :])
         nc.sync.dma_start(out=q_sb[:, 1:4, :], in_=q_view[:, 1:4, :])
-        nc.sync.dma_start(out=v_sb[:], in_=v.rearrange("(g c t) h d -> c g t (h d)", g=2, t=4))
+        v_view = v.rearrange("(g c t) h d -> c g t (h d)", g=2, t=4)
+        nc.sync.dma_start(out=v_sb[:, 0], in_=v_view[:, 0])
         for u in range(2):
             for e in range(2):
                 nc.sync.dma_start(out=k_sb[e:P:2, 1, 2 * u:2 * u + 2, :], in_=k_view[1, e, u])
+        nc.sync.dma_start(out=q_sb[:, 8:12, :], in_=q_view[:, 8:12, :])
         nc.sync.dma_start(out=w_sb[:], in_=W_proj.rearrange("(a p) f -> p a f", p=P))
-        for a in chunk_order[1:]:
+        nc.sync.dma_start(out=v_sb[:, 1], in_=v_view[:, 1])
+        for a in chunk_order[2:]:
             nc.sync.dma_start(out=q_sb[:, 4 * a:4 * a + 4, :], in_=q_view[:, 4 * a:4 * a + 4, :])
 
         ident = const.tile([P, P], BF16, name="ident")
@@ -189,8 +192,18 @@ def tile_mha_t_kernel(tc, q, k, v, W_proj, out):
             src = st[("pt", u)][:, 0:np_ * 256].rearrange("p (g u q) -> p g q u", g=np_, u=2)
             nc.scalar.copy(out=gr[:, h % 2], in_=src)
 
+        def e_quant_last(u):
+            gi, h = u // 4, u % 4
+            nc.vector.quantize_mx(
+                out=st[("cod", gi)][:, h].rearrange("p g q -> p (g q)").bitcast(FP8X4),
+                scales=st[("sca", gi)][:, h].rearrange("p g q -> p (g q)"),
+                in_=st[("gr", u // 2)][:, h % 2].rearrange("p g q u -> p (g q u)").bitcast(BF16))
+
         def e_quant(u):
             i, h = unit(u)
+            if u == n_units - 1:
+                e_quant_last(u)
+                return
             np_ = passes(i)
             if h == 1:
                 st[("cod", u // 4)] = work.tile([P, H, np_, P], U32, name="cod", tag="cod", align_bytes=64)
@@ -207,11 +220,15 @@ def tile_mha_t_kernel(tc, q, k, v, W_proj, out):
             np_ = passes(i)
             cod = st[("cod", gi)]
             sca = st[("sca", gi)]
-            o = psum.tile([P, E], F32, name="o", tag="x")
+            halves = 2 if gi == n_groups - 1 else 1
+            o = []
+            for b in range(halves):
+                bank = psum.tile([P, E], F32, name="o", tag="x")
+                o.append(bank)
             for h in range(H):
                 for g in range(np_):
                     nc.tensor.matmul_mx(
-                        out=o[:, h * D:(h + 1) * D],
+                        out=o[h * halves // H][:, h * D:(h + 1) * D],
                         lhsT=cod[:, h, g, :].bitcast(FP8X4), lhsT_scale=sca[:, h, g, :],
                         rhs=vcod[:, g, h * D:(h + 1) * D].bitcast(FP8X4), rhs_scale=vsca[:, g, h * D:(h + 1) * D],
                         start=(g == 0), stop=(g == np_ - 1))
@@ -233,8 +250,12 @@ def tile_mha_t_kernel(tc, q, k, v, W_proj, out):
 
         def norm(gi):
             ob = work.tile([P, H, D], BF16, name="ob", tag="ob")
-            nc.vector.tensor_tensor(out=ob[:], in0=st[("o", gi)][:].rearrange("p (h d) -> p h d", h=H),
-                                    in1=st[("rinv", gi)][:].unsqueeze(2).to_broadcast([P, H, D]), op=ALU.mult)
+            o, rinv = st[("o", gi)], st[("rinv", gi)]
+            hv = H // len(o)
+            nc.vector.tensor_tensor(out=ob[:, 0:hv], in0=o[0][:].rearrange("p (h d) -> p h d", h=H)[:, 0:hv],
+                                    in1=rinv[:, 0:hv].unsqueeze(2).to_broadcast([P, hv, D]), op=ALU.mult)
+            for h in range(hv, H):
+                nc.scalar.activation(out=ob[:, h], in_=o[1][:, h * D:(h + 1) * D], func=ACTF.Copy, scale=rinv[:, h:h + 1])
             st[("ob", gi)] = ob
 
         def o_transposes(gi):
@@ -258,23 +279,36 @@ def tile_mha_t_kernel(tc, q, k, v, W_proj, out):
             st[("osca", gi)] = osca
 
         def proj(gi):
-            y = psum.tile([P, E], F32, name="y", tag="x")
-            nc.tensor.matmul_mx(out=y[:], lhsT=st[("ocod", gi)][:].bitcast(FP8X4), lhsT_scale=st[("osca", gi)][:],
-                                rhs=wcod[:].bitcast(FP8X4), rhs_scale=wsca[:], start=True, stop=True)
-            st[("y", gi)] = y
+            parts = 2 if gi == n_groups - 1 else 1
+            n = E // parts
+            st[("y", gi)] = []
+            for b in range(parts):
+                y = psum.tile([P, E], F32, name="y", tag="x")
+                nc.tensor.matmul_mx(out=y[:, 0:n], lhsT=st[("ocod", gi)][:].bitcast(FP8X4), lhsT_scale=st[("osca", gi)][:],
+                                    rhs=wcod[:, b * n:(b + 1) * n].bitcast(FP8X4), rhs_scale=wsca[:, b * n:(b + 1) * n],
+                                    start=True, stop=True)
+                st[("y", gi)].append(y)
 
         def y_out(gi):
             i = GROUP_ORDER[gi]
-            ysb = work.tile([P, E], F32, name="ysb", tag="ysb", bufs=32)
-            nc.vector.tensor_copy(out=ysb[:], in_=st[("y", gi)][:])
-            nc.sync.dma_start(out=out[i * P:(i + 1) * P, :], in_=ysb[:])
+            n = E // len(st[("y", gi)])
+            for b, y in enumerate(st[("y", gi)]):
+                ysb = work.tile([P, n], F32, name="ysb", tag="ysb", bufs=33)
+                if b == 0:
+                    nc.vector.tensor_copy(out=ysb[:], in_=y[:, 0:n])
+                    nc.sync.dma_start(out=out[i * P:(i + 1) * P, 0:n], in_=ysb[:])
+                else:
+                    nc.scalar.copy(out=ysb[:], in_=y[:, 0:n])
+                    nc.scalar.dma_start(out=out[i * P:(i + 1) * P, n:E], in_=ysb[:])
 
-        def w_transposes(a):
-            words = w_sb[:, a, :].bitcast(F32)
-            pw = psum.tile([P, 2 * P], F32, name="pw", tag="x")
-            for u in range(2):
-                nc.tensor.transpose(pw[:, u * P:(u + 1) * P], words[:, u:2 * P:2], ident_w[:])
-            nc.scalar.copy(out=wg[:, a * P:(a + 1) * P, :], in_=pw[:].rearrange("p (u o) -> p o u", u=2))
+        def w_transposes(half):
+            pw = psum.tile([P, 2, 2, P], F32, name="pw", tag="x")
+            for b in range(2):
+                words = w_sb[:, 2 * half + b, :].bitcast(F32)
+                for u in range(2):
+                    nc.tensor.transpose(pw[:, b, u, :], words[:, u:2 * P:2], ident_w[:])
+            nc.scalar.copy(out=wg[:, half * 2 * P:(half + 1) * 2 * P, :].rearrange("p (b o) u -> p b o u", b=2),
+                           in_=pw[:].rearrange("p b u o -> p b o u"))
 
         def v_regroup(g, piece):
             f0 = 128 * piece
@@ -310,8 +344,8 @@ def tile_mha_t_kernel(tc, q, k, v, W_proj, out):
                 qt_transposes(group(-5))
             if at(10):
                 o_transposes(group(10))
-            if s in (5, 8, 9, 12):
-                w_transposes((5, 8, 9, 12).index(s))
+            if s in (9, 12):
+                w_transposes((9, 12).index(s))
             if 0 <= s - 1 < n_units:
                 e_transposes(s - 1)
             scores(s + 3, (0,))
@@ -331,9 +365,11 @@ def tile_mha_t_kernel(tc, q, k, v, W_proj, out):
                 recip(group(7))
             if s % 2 == 0 and 0 <= s - 3 < n_units:
                 e_quant(s - 3)
+            if s == n_units + 1:
+                e_quant_last(n_units - 2)
             if s == 5:
                 v_quant(0)
-            if s == 15:
+            if s == 19:
                 v_quant(1)
             if s == 13:
                 nc.vector.quantize_mx(out=wcod[:].bitcast(FP8X4), scales=wsca[:],
@@ -348,5 +384,5 @@ def tile_mha_t_kernel(tc, q, k, v, W_proj, out):
             neg_max(s + 2)
             if 0 <= s < 4:
                 v_regroup(0, s)
-            if 8 <= s < 12:
-                v_regroup(1, s - 8)
+            if 12 <= s < 16:
+                v_regroup(1, s - 12)

@@ -21,6 +21,7 @@ P = 128
 SCALE = 1.0 / math.sqrt(D)
 MASK_FILL = -131072.0
 GROUP_ORDER = list(range(0, 4)) + list(range(8, 32)) + list(range(7, 3, -1))
+N_PAIRED = 28
 
 
 def tile_mha_t_kernel(tc, q, k, v, W_proj, out):
@@ -37,12 +38,15 @@ def tile_mha_t_kernel(tc, q, k, v, W_proj, out):
         q_sb = const.tile([P, 32, E], BF16, name="q_sb")
         q_view = q.rearrange("(i p) h d -> p i (h d)", p=P)
         k_view = k.rearrange("(g a c u e) h d -> g e u c a (h d)", g=2, a=2, u=2, e=2)
-        chunk_order = [0, 2, 3, 4, 5, 6, 7, 1]
-        for u in range(2):
-            for e in range(2):
-                nc.sync.dma_start(out=k_sb[e:P:2, 0, 2 * u:2 * u + 2, :], in_=k_view[0, e, u])
-        nc.sync.dma_start(out=q_sb[:, 0:1, :], in_=q_view[:, 0:1, :])
-        nc.sync.dma_start(out=q_sb[:, 1:4, :], in_=q_view[:, 1:4, :])
+        for c in range(2):
+            cols = slice(c * 2 * D, (c + 1) * 2 * D)
+            for u in range(2):
+                for e in range(2):
+                    nc.sync.dma_start(out=k_sb[e:P:2, 0, 2 * u:2 * u + 2, cols], in_=k_view[0, e, u, :, :, cols])
+            if c == 0:
+                nc.sync.dma_start(out=q_sb[:, 0:1, :], in_=q_view[:, 0:1, :])
+                nc.sync.dma_start(out=q_sb[:, 1:2, :], in_=q_view[:, 1:2, :])
+        nc.sync.dma_start(out=q_sb[:, 2:4, :], in_=q_view[:, 2:4, :])
         v_view = v.rearrange("(g c t) h d -> c g t (h d)", g=2, t=4)
         nc.sync.dma_start(out=v_sb[:, 0], in_=v_view[:, 0])
         for u in range(2):
@@ -51,8 +55,10 @@ def tile_mha_t_kernel(tc, q, k, v, W_proj, out):
         nc.sync.dma_start(out=q_sb[:, 8:12, :], in_=q_view[:, 8:12, :])
         nc.sync.dma_start(out=w_sb[:], in_=W_proj.rearrange("(a p) f -> p a f", p=P))
         nc.sync.dma_start(out=v_sb[:, 1], in_=v_view[:, 1])
-        for a in chunk_order[2:]:
-            nc.sync.dma_start(out=q_sb[:, 4 * a:4 * a + 4, :], in_=q_view[:, 4 * a:4 * a + 4, :])
+
+        def q_loads(blocks):
+            for a in blocks:
+                nc.sync.dma_start(out=q_sb[:, 4 * a:4 * a + 4, :], in_=q_view[:, 4 * a:4 * a + 4, :])
 
         ident = const.tile([P, P], BF16, name="ident")
         make_identity(nc, ident[:])
@@ -69,12 +75,17 @@ def tile_mha_t_kernel(tc, q, k, v, W_proj, out):
         vg = const.tile([P, 2, E, 4], BF16, name="vg", align_bytes=64)
         vcod = const.tile([P, 2, E], U32, name="vcod", align_bytes=64)
         vsca = const.tile([P, 2, E], U8, name="vsca", align_bytes=64)
-        wg = const.tile([P, E, 2], F32, name="wg", align_bytes=64)
+        wg = const.tile([P, E, H], BF16, name="wg", align_bytes=64)
         wcod = const.tile([P, E], U32, name="wcod", align_bytes=64)
         wsca = const.tile([P, E], U8, name="wsca", align_bytes=64)
         warm = const.tile([P, 1], F32, name="warm")
         nc.vector.memset(warm[:], 0.0)
         warm_out = const.tile([P, 1], F32, name="warm_out")
+        e_light = []
+        for j in range(4):
+            e_tile = const.tile([P, 512], BF16, name="e_light%d" % j)
+            nc.gpsimd.memset(e_tile[:], 0.0)
+            e_light.append(e_tile)
 
         ctx.enter_context(tc.manual_schedule())
         nc.scalar.activation(out=warm_out[:], in_=warm[:], func=ACTF.Exp)
@@ -106,17 +117,23 @@ def tile_mha_t_kernel(tc, q, k, v, W_proj, out):
         def unit(u):
             return GROUP_ORDER[u // 4], u % 4
 
+        def q_tiles(gj):
+            return (gj,) if gj < 2 else (gj, gj + 1)
+
         def qt_transposes(gj):
-            i = GROUP_ORDER[gj]
-            pq = psum.tile([P, E], BF16, name="pq", tag="x")
-            for h in range(H):
-                nc.tensor.transpose(pq[:, h * P:(h + 1) * P], q_sb[:, i, h * D:(h + 1) * D], ident[:])
+            tiles = q_tiles(gj)
+            pq = psum.tile([P, len(tiles), E], BF16, name="pq", tag="x")
+            for b, g in enumerate(tiles):
+                for h in range(H):
+                    nc.tensor.transpose(pq[:, b, h * P:(h + 1) * P], q_sb[:, GROUP_ORDER[g], h * D:(h + 1) * D], ident[:])
             st[("pq", gj)] = pq
 
         def qt_copy(gj):
-            qT = work.tile([P, E], BF16, name="qT", tag="qT")
+            tiles = q_tiles(gj)
+            qT = work.tile([P, len(tiles), E], BF16, name="qT", tag="qT")
             nc.vector.tensor_copy(out=qT[:], in_=st[("pq", gj)][:])
-            st[("qT", gj)] = qT
+            for b, g in enumerate(tiles):
+                st[("qT", g)] = qT[:, b, :]
 
         def scores(u, gs):
             if not 0 <= u < n_units:
@@ -160,19 +177,25 @@ def tile_mha_t_kernel(tc, q, k, v, W_proj, out):
                                         op0=ALU.mult, op1=ALU.add)
             st[("nb", u)] = nb
 
+        def in_group(gi):
+            return 2 if gi < N_PAIRED else 1
+
         def exps(u):
             i, h = unit(u)
-            if h == 0:
-                st[("rs", u // 4)] = small.tile([P, H, 2], F32, name="rs", tag="rs")
-            rs = st[("rs", u // 4)]
-            e = work.tile([P, T], BF16, name="e", tag="e")
+            gi = u // 4
+            n_in = in_group(gi)
+            if h == 0 and gi % n_in == 0:
+                st[("rs", gi)] = small.tile([P, n_in * H, 2], F32, name="rs", tag="rs")
+            rs = st[("rs", gi - gi % n_in)]
+            col = gi % n_in * H + h
+            e = e_light[u % 4] if i < 4 else work.tile([P, T], BF16, name="e", tag="e")
             for g in range(passes(i)):
                 eg = e[:, g * 512:(g + 1) * 512]
                 n_live = live_cols(i, g)
-                if n_live < P:
+                if n_live < P and i >= 4:
                     nc.gpsimd.memset(eg.rearrange("p (u w) -> p u w", u=2)[:, :, 2 * n_live:2 * P], 0.0)
                 nc.scalar.activation(out=live(eg, i, g), in_=live(st[("s", u)][g][:], i, g), func=ACTF.Exp,
-                                     bias=st[("nb", u)][:], scale=SCALE, accum_out=rs[:, h, g:g + 1])
+                                     bias=st[("nb", u)][:], scale=SCALE, accum_out=rs[:, col, g:g + 1])
             st[("e", u)] = e
 
         def e_transposes(u):
@@ -186,97 +209,91 @@ def tile_mha_t_kernel(tc, q, k, v, W_proj, out):
         def e_copy(u):
             i, h = unit(u)
             np_ = passes(i)
-            if h % 2 == 0:
-                st[("gr", u // 2)] = work.tile([P, 2, np_, P, 2], F32, name="gr", tag="gr", align_bytes=64)
-            gr = st[("gr", u // 2)]
+            if h == 0:
+                st[("gr", u // 4)] = work.tile([P, H, np_, P, 2], F32, name="gr", tag="gr", bufs=3, align_bytes=64)
+            gr = st[("gr", u // 4)]
             src = st[("pt", u)][:, 0:np_ * 256].rearrange("p (g u q) -> p g q u", g=np_, u=2)
-            nc.scalar.copy(out=gr[:, h % 2], in_=src)
+            nc.scalar.copy(out=gr[:, h], in_=src)
 
-        def e_quant_last(u):
-            gi, h = u // 4, u % 4
+        def e_quant(gi, h0, h1):
+            np_ = passes(GROUP_ORDER[gi])
+            if h0 == 0:
+                st[("cod", gi)] = work.tile([P, H, np_, P], U32, name="cod", tag="cod", bufs=6, align_bytes=64)
+                st[("sca", gi)] = work.tile([P, H, np_, P], U8, name="sca", tag="sca", bufs=6, align_bytes=64)
             nc.vector.quantize_mx(
-                out=st[("cod", gi)][:, h].rearrange("p g q -> p (g q)").bitcast(FP8X4),
-                scales=st[("sca", gi)][:, h].rearrange("p g q -> p (g q)"),
-                in_=st[("gr", u // 2)][:, h % 2].rearrange("p g q u -> p (g q u)").bitcast(BF16))
+                out=st[("cod", gi)][:, h0:h1].rearrange("p h g q -> p (h g q)").bitcast(FP8X4),
+                scales=st[("sca", gi)][:, h0:h1].rearrange("p h g q -> p (h g q)"),
+                in_=st[("gr", gi)][:, h0:h1].rearrange("p h g q u -> p (h g q u)").bitcast(BF16))
 
-        def e_quant(u):
-            i, h = unit(u)
-            if u == n_units - 1:
-                e_quant_last(u)
-                return
-            np_ = passes(i)
-            if h == 1:
-                st[("cod", u // 4)] = work.tile([P, H, np_, P], U32, name="cod", tag="cod", align_bytes=64)
-                st[("sca", u // 4)] = work.tile([P, H, np_, P], U8, name="sca", tag="sca", align_bytes=64)
-            cod = st[("cod", u // 4)]
-            sca = st[("sca", u // 4)]
-            nc.vector.quantize_mx(
-                out=cod[:, h - 1:h + 1].rearrange("p h g q -> p (h g q)").bitcast(FP8X4),
-                scales=sca[:, h - 1:h + 1].rearrange("p h g q -> p (h g q)"),
-                in_=st[("gr", u // 2)][:].rearrange("p h g q u -> p (h g q u)").bitcast(BF16))
-
-        def av(gi):
-            i = GROUP_ORDER[gi]
-            np_ = passes(i)
+        def av(gi, h0=0, h1=H):
+            np_ = passes(GROUP_ORDER[gi])
             cod = st[("cod", gi)]
             sca = st[("sca", gi)]
-            halves = 2 if gi == n_groups - 1 else 1
-            o = []
-            for b in range(halves):
-                bank = psum.tile([P, E], F32, name="o", tag="x")
-                o.append(bank)
-            for h in range(H):
+            if h0 == 0:
+                o_bank = psum.tile([P, H, P], F32, name="o", tag="x")
+                st[("o", gi)] = o_bank
+            o = st[("o", gi)]
+            for h in range(h0, h1):
                 for g in range(np_):
                     nc.tensor.matmul_mx(
-                        out=o[h * halves // H][:, h * D:(h + 1) * D],
-                        lhsT=cod[:, h, g, :].bitcast(FP8X4), lhsT_scale=sca[:, h, g, :],
-                        rhs=vcod[:, g, h * D:(h + 1) * D].bitcast(FP8X4), rhs_scale=vsca[:, g, h * D:(h + 1) * D],
+                        out=o[:, h, :],
+                        lhsT=vcod[:, g, h * D:(h + 1) * D].bitcast(FP8X4), lhsT_scale=vsca[:, g, h * D:(h + 1) * D],
+                        rhs=cod[:, h, g, :].bitcast(FP8X4), rhs_scale=sca[:, h, g, :],
                         start=(g == 0), stop=(g == np_ - 1))
-            st[("o", gi)] = o
 
         def row_sums(gi):
             rs = st[("rs", gi)]
             if passes(GROUP_ORDER[gi]) == 2:
-                rsum = small.tile([P, H], F32, name="rsum", tag="rsum")
+                rsum = small.tile([P, in_group(gi) * H], F32, name="rsum", tag="rsum")
                 nc.gpsimd.tensor_tensor(out=rsum[:], in0=rs[:, :, 0], in1=rs[:, :, 1], op=ALU.add)
                 st[("rsum", gi)] = rsum[:]
             else:
                 st[("rsum", gi)] = rs[:, :, 0]
 
         def recip(gi):
-            rinv = small.tile([P, H], F32, name="rinv", tag="rinv")
+            rinv = small.tile([P, in_group(gi) * H], F32, name="rinv", tag="rinv")
             nc.vector.reciprocal(out=rinv[:], in_=st[("rsum", gi)])
             st[("rinv", gi)] = rinv
 
+        def rinv_through_out(gi):
+            i = GROUP_ORDER[gi]
+            rows = out[i * P:i * P + 2, :].rearrange("a b -> (a b)")
+            nc.sync.dma_start(out=rows.rearrange("(q c) -> q c", c=2 * H), in_=st[("rinv", gi)][:])
+            rb = work.tile([P, P, 2, H], F32, name="rb", tag="rb", bufs=3)
+            nc.sync.dma_start(out=rb[:].rearrange("p q b h -> p (q b h)"), in_=rows.partition_broadcast(P))
+            for b in range(2):
+                st[("rb", gi + b)] = rb[:, :, b, :]
+
+        def rinv_matmul(gi):
+            pr = psum.tile([P, H, P], F32, name="pr", tag="x")
+            for h in range(H):
+                nc.tensor.matmul(pr[:, h, :], lhsT=st[("rinv", gi)][:, h:h + 1].to_broadcast([P, P]), rhs=ident_w[:],
+                                 start=True, stop=True)
+            st[("pr", gi)] = pr
+
+        def rinv_copy(gi):
+            rb = work.tile([P, H, P], F32, name="rb1", tag="rb1", bufs=2)
+            nc.scalar.copy(out=rb[:], in_=st[("pr", gi)][:])
+            st[("rb", gi)] = rb[:].rearrange("p h q -> p q h")
+
         def norm(gi):
-            ob = work.tile([P, H, D], BF16, name="ob", tag="ob")
-            o, rinv = st[("o", gi)], st[("rinv", gi)]
-            hv = H // len(o)
-            nc.vector.tensor_tensor(out=ob[:, 0:hv], in0=o[0][:].rearrange("p (h d) -> p h d", h=H)[:, 0:hv],
-                                    in1=rinv[:, 0:hv].unsqueeze(2).to_broadcast([P, hv, D]), op=ALU.mult)
-            for h in range(hv, H):
-                nc.scalar.activation(out=ob[:, h], in_=o[1][:, h * D:(h + 1) * D], func=ACTF.Copy, scale=rinv[:, h:h + 1])
-            st[("ob", gi)] = ob
-
-        def o_transposes(gi):
-            words = st[("ob", gi)][:].rearrange("p h d -> p (h d)").bitcast(F32)
-            po = psum.tile([P, 2 * P], F32, name="po", tag="x")
-            for u in range(2):
-                nc.tensor.transpose(po[:, u * P:(u + 1) * P], words[:, u:2 * P:2], ident_w[:])
-            st[("po", gi)] = po
-
-        def o_copy(gi):
-            og = work.tile([P, P, 2], F32, name="og", tag="og", align_bytes=64)
-            nc.scalar.copy(out=og[:], in_=st[("po", gi)][:].rearrange("p (u q) -> p q u", u=2))
-            st[("og", gi)] = og
+            n_in = in_group(gi)
+            if gi % n_in == 0:
+                st[("og", gi)] = work.tile([P, n_in, P, H], BF16, name="og", tag="og", align_bytes=64)
+            og = st[("og", gi - gi % n_in)]
+            nc.vector.tensor_tensor(out=og[:, gi % n_in], in0=st[("o", gi)][:].rearrange("p h q -> p q h"),
+                                    in1=st[("rb", gi)], op=ALU.mult)
 
         def o_quant(gi):
-            ocod = work.tile([P, P], U32, name="ocod", tag="ocod", align_bytes=64)
-            osca = work.tile([P, P], U8, name="osca", tag="osca", align_bytes=64)
-            nc.vector.quantize_mx(out=ocod[:].bitcast(FP8X4), scales=osca[:],
-                                  in_=st[("og", gi)][:].rearrange("p q u -> p (q u)").bitcast(BF16))
-            st[("ocod", gi)] = ocod
-            st[("osca", gi)] = osca
+            n_in = in_group(gi)
+            ocod = work.tile([P, n_in, P], U32, name="ocod", tag="ocod", align_bytes=64)
+            osca = work.tile([P, n_in, P], U8, name="osca", tag="osca", align_bytes=64)
+            nc.vector.quantize_mx(out=ocod[:].rearrange("p b q -> p (b q)").bitcast(FP8X4),
+                                  scales=osca[:].rearrange("p b q -> p (b q)"),
+                                  in_=st[("og", gi)][:].rearrange("p b q h -> p (b q h)"))
+            for b in range(n_in):
+                st[("ocod", gi + b)] = ocod[:, b, :]
+                st[("osca", gi + b)] = osca[:, b, :]
 
         def proj(gi):
             parts = 2 if gi == n_groups - 1 else 1
@@ -284,31 +301,33 @@ def tile_mha_t_kernel(tc, q, k, v, W_proj, out):
             st[("y", gi)] = []
             for b in range(parts):
                 y = psum.tile([P, E], F32, name="y", tag="x")
-                nc.tensor.matmul_mx(out=y[:, 0:n], lhsT=st[("ocod", gi)][:].bitcast(FP8X4), lhsT_scale=st[("osca", gi)][:],
+                nc.tensor.matmul_mx(out=y[:, 0:n], lhsT=st[("ocod", gi)].bitcast(FP8X4), lhsT_scale=st[("osca", gi)],
                                     rhs=wcod[:, b * n:(b + 1) * n].bitcast(FP8X4), rhs_scale=wsca[:, b * n:(b + 1) * n],
                                     start=True, stop=True)
                 st[("y", gi)].append(y)
+
+        def y_on_scalar(gi):
+            return gi % 4 == 3 if gi < N_PAIRED else gi in (n_groups - 3, n_groups - 2)
 
         def y_out(gi):
             i = GROUP_ORDER[gi]
             n = E // len(st[("y", gi)])
             for b, y in enumerate(st[("y", gi)]):
-                ysb = work.tile([P, n], F32, name="ysb", tag="ysb", bufs=33)
-                if b == 0:
-                    nc.vector.tensor_copy(out=ysb[:], in_=y[:, 0:n])
-                    nc.sync.dma_start(out=out[i * P:(i + 1) * P, 0:n], in_=ysb[:])
-                else:
+                ysb = work.tile([P, n], F32, name="ysb", tag="ysb", bufs=16)
+                if y_on_scalar(gi) or b == 1:
                     nc.scalar.copy(out=ysb[:], in_=y[:, 0:n])
-                    nc.scalar.dma_start(out=out[i * P:(i + 1) * P, n:E], in_=ysb[:])
+                else:
+                    nc.vector.tensor_copy(out=ysb[:], in_=y[:, 0:n])
+                queue = nc.scalar if b == 1 else nc.sync
+                queue.dma_start(out=out[i * P:(i + 1) * P, b * n:(b + 1) * n], in_=ysb[:])
 
         def w_transposes(half):
-            pw = psum.tile([P, 2, 2, P], F32, name="pw", tag="x")
+            pw = psum.tile([P, 2, H, P], BF16, name="pw", tag="x")
             for b in range(2):
-                words = w_sb[:, 2 * half + b, :].bitcast(F32)
-                for u in range(2):
-                    nc.tensor.transpose(pw[:, b, u, :], words[:, u:2 * P:2], ident_w[:])
-            nc.scalar.copy(out=wg[:, half * 2 * P:(half + 1) * 2 * P, :].rearrange("p (b o) u -> p b o u", b=2),
-                           in_=pw[:].rearrange("p b u o -> p b o u"))
+                for h in range(H):
+                    nc.tensor.transpose(pw[:, b, h, :], w_sb[:, 2 * half + b, h * P:(h + 1) * P], ident[:])
+            nc.scalar.copy(out=wg[:, half * 2 * P:(half + 1) * 2 * P, :].rearrange("p (b o) h -> p b o h", b=2),
+                           in_=pw[:].rearrange("p b h o -> p b o h"))
 
         def v_regroup(g, piece):
             f0 = 128 * piece
@@ -325,64 +344,102 @@ def tile_mha_t_kernel(tc, q, k, v, W_proj, out):
         kt_transposes(0, 1)
         kt_transposes(0, 2)
 
-        for s in range(-3, n_units + 15):
-            def at(offset):
-                return (s - offset) % 4 == 0 and 0 <= (s - offset) // 4 < n_groups
+        def single(s, offset):
+            gi = (s - offset) // 4
+            return gi if (s - offset) % 4 == 0 and N_PAIRED <= gi < n_groups else None
 
-            def group(offset):
-                return (s - offset) // 4
+        def paired(s, offset, b=0):
+            gi = (s - offset) // 4
+            return gi + b if (s - offset) % 8 == 0 and 0 <= gi < N_PAIRED else None
 
+        def run(fn, *tiles):
+            for gi in tiles:
+                if gi is not None:
+                    fn(gi)
+
+        last = n_groups - 1
+
+        def results_due(s):
+            due = [paired(s, 27), paired(s, 31, 1)]
+            if s == n_units + 10:
+                due += [last - 1, last]
+            elif single(s, 14) != last - 1:
+                due += [single(s, 14)]
+            return [gi for gi in due if gi is not None]
+
+        next_scores = 0
+        next_max = 0
+        for s in range(-3, n_units + 11):
+            one = [None if single(s, d) == last else single(s, d) for d in range(11)]
+            if s >= 0:
+                run(rinv_matmul, one[7])
+                run(rinv_copy, one[7])
             if 0 <= s < n_units:
                 exps(s)
             if s == -2:
                 kt_transposes(0, 3)
             if 13 <= s < 17:
                 kt_transposes(1, s - 13)
-            if at(14):
-                proj(group(14))
-            if at(-5) and group(-5) > 0:
-                qt_transposes(group(-5))
-            if at(10):
-                o_transposes(group(10))
-            if s in (9, 12):
-                w_transposes((9, 12).index(s))
+            due = results_due(s)
+            while next_scores < n_units and next_scores <= s + (3 if passes(unit(next_scores)[0]) == 1 else 2):
+                scores(next_scores, (0,))
+                next_scores += 1
+            q_next = (s + 6) // 4
+            q_due = (s + 6) % 4 == 0 and (q_next == 1 or (1 < q_next < n_groups and q_next % 2 == 0))
+            if q_due:
+                qt_transposes(q_next)
+            if s in (21, 24):
+                w_transposes((21, 24).index(s))
+            run(proj, *due)
             if 0 <= s - 1 < n_units:
                 e_transposes(s - 1)
-            scores(s + 3, (0,))
+            if s == n_units + 1:
+                rinv_matmul(last)
             scores(s + 2, (1,))
-            if at(7):
-                av(group(7))
+            run(av, paired(s, 20), paired(s, 24, 1), one[7])
+            if s == n_units + 2:
+                av(last, 0, 3)
+            if s == n_units + 3:
+                av(last, 3, 4)
             if 0 <= s - 1 < n_units:
                 e_copy(s - 1)
-            if at(10):
-                o_copy(group(10))
-            if at(14):
-                y_out(group(14))
-            if at(9):
-                norm(group(9))
-            maxs(s + 2, 0)
-            if at(7):
-                recip(group(7))
-            if s % 2 == 0 and 0 <= s - 3 < n_units:
-                e_quant(s - 3)
+            if s == n_units + 2:
+                rinv_copy(last)
+            run(y_out, *[gi for gi in due if y_on_scalar(gi)])
+            if s == n_units:
+                row_sums(last)
+                recip(last)
+            run(recip, paired(s, 10), one[6])
+            run(rinv_through_out, paired(s, 10))
+            if s == 10:
+                q_loads((3, 4, 5, 6, 7, 1))
+            run(norm, paired(s, 21), paired(s, 25, 1), single(s, 8))
+            maxed = []
+            while next_max < n_units and next_max <= s + (3 if passes(unit(next_max)[0]) == 1 else 2):
+                maxs(next_max, 0)
+                maxed.append(next_max)
+                next_max += 1
+            run(y_out, *[gi for gi in due if not y_on_scalar(gi)])
+            if q_due:
+                qt_copy(q_next)
+            run(o_quant, paired(s, 26), single(s, 10))
+            if s % 2 == 0 and 0 <= s - 4 < n_units - 2:
+                e_quant((s - 4) // 4, (s - 4) % 4, (s - 4) % 4 + 2)
             if s == n_units + 1:
-                e_quant_last(n_units - 2)
-            if s == 5:
+                e_quant(last, 2, 3)
+            if s == n_units + 2:
+                e_quant(last, 3, 4)
+            if s == 11:
                 v_quant(0)
-            if s == 19:
+            if s == 20:
                 v_quant(1)
-            if s == 13:
-                nc.vector.quantize_mx(out=wcod[:].bitcast(FP8X4), scales=wsca[:],
-                                      in_=wg[:].rearrange("p o u -> p (o u)").bitcast(BF16))
-            if at(-5) and group(-5) > 0:
-                qt_copy(group(-5))
-            if at(12):
-                o_quant(group(12))
+            if s == 26:
+                nc.vector.quantize_mx(out=wcod[:].bitcast(FP8X4), scales=wsca[:], in_=wg[:].rearrange("p o h -> p (o h)"))
             maxs(s + 2, 1)
-            if at(5):
-                row_sums(group(5))
-            neg_max(s + 2)
-            if 0 <= s < 4:
-                v_regroup(0, s)
-            if 12 <= s < 16:
-                v_regroup(1, s - 12)
+            run(row_sums, paired(s, 9), one[5])
+            for u in maxed:
+                neg_max(u)
+            if 6 <= s < 10:
+                v_regroup(0, s - 6)
+            if 14 <= s < 18:
+                v_regroup(1, s - 14)

@@ -20,7 +20,7 @@ AX = mybir.AxisListType
 P = 128
 SCALE = 1.0 / math.sqrt(D)
 MASK_FILL = -131072.0
-GROUP_ORDER = list(range(0, 4)) + list(range(8, 32)) + list(range(7, 3, -1))
+GROUP_ORDER = list(range(0, 4)) + list(range(8, 20)) + list(range(7, 3, -1)) + list(range(20, 32))
 N_PAIRED = 28
 
 
@@ -98,7 +98,7 @@ def tile_mha_t_kernel(tc, q, k, v, W_proj, out):
             pk = psum.tile([P, 512], BF16, name="pk", tag="x")
             for t in range(4):
                 nc.tensor.transpose(pk[:, t * P:(t + 1) * P], k_sb[:, g, t, h * D:(h + 1) * D], ident[:])
-            if (g, h) in ((0, 0), (1, 1), (1, 3)):
+            if (g, h) in ((0, 0), (0, 1), (1, 2), (1, 3)):
                 nc.vector.tensor_copy(out=kT[:, g, h, :], in_=pk[:])
             else:
                 nc.scalar.copy(out=kT[:, g, h, :], in_=pk[:])
@@ -267,8 +267,7 @@ def tile_mha_t_kernel(tc, q, k, v, W_proj, out):
         def rinv_matmul(gi):
             pr = psum.tile([P, H, P], F32, name="pr", tag="x")
             for h in range(H):
-                nc.tensor.matmul(pr[:, h, :], lhsT=st[("rinv", gi)][:, h:h + 1].to_broadcast([P, P]), rhs=ident_w[:],
-                                 start=True, stop=True)
+                nc.tensor.transpose(pr[:, h, :], st[("rinv", gi)][:, h:h + 1].to_broadcast([P, P]), ident_w[:])
             st[("pr", gi)] = pr
 
         def rinv_copy(gi):
@@ -307,7 +306,7 @@ def tile_mha_t_kernel(tc, q, k, v, W_proj, out):
                 st[("y", gi)].append(y)
 
         def y_on_scalar(gi):
-            return gi % 4 == 3 if gi < N_PAIRED else gi in (n_groups - 3, n_groups - 2)
+            return gi % 4 == 3 if gi < N_PAIRED - 2 else gi in (27, 29)
 
         def y_out(gi):
             i = GROUP_ORDER[gi]
@@ -360,21 +359,14 @@ def tile_mha_t_kernel(tc, q, k, v, W_proj, out):
         last = n_groups - 1
 
         def results_due(s):
-            due = [paired(s, 27), paired(s, 31, 1)]
-            if s == n_units + 10:
-                due += [last - 1, last]
-            elif single(s, 14) != last - 1:
-                due += [single(s, 14)]
-            return [gi for gi in due if gi is not None]
+            return [gi for gi in (paired(s, 23), paired(s, 27, 1), single(s, 14)) if gi is not None]
 
         next_scores = 0
         next_max = 0
-        for s in range(-3, n_units + 11):
-            one = [None if single(s, d) == last else single(s, d) for d in range(11)]
+        for s in range(-3, n_units):
+            run(rinv_matmul, single(s, 7))
+            run(rinv_copy, single(s, 7))
             if s >= 0:
-                run(rinv_matmul, one[7])
-                run(rinv_copy, one[7])
-            if 0 <= s < n_units:
                 exps(s)
             if s == -2:
                 kt_transposes(0, 3)
@@ -388,32 +380,21 @@ def tile_mha_t_kernel(tc, q, k, v, W_proj, out):
             q_due = (s + 6) % 4 == 0 and (q_next == 1 or (1 < q_next < n_groups and q_next % 2 == 0))
             if q_due:
                 qt_transposes(q_next)
-            if s in (21, 24):
-                w_transposes((21, 24).index(s))
+            if s in (17, 19):
+                w_transposes((17, 19).index(s))
             run(proj, *due)
-            if 0 <= s - 1 < n_units:
+            if s >= 1:
                 e_transposes(s - 1)
-            if s == n_units + 1:
-                rinv_matmul(last)
             scores(s + 2, (1,))
-            run(av, paired(s, 20), paired(s, 24, 1), one[7])
-            if s == n_units + 2:
-                av(last, 0, 3)
-            if s == n_units + 3:
-                av(last, 3, 4)
-            if 0 <= s - 1 < n_units:
+            run(av, paired(s, 16), paired(s, 20, 1), single(s, 7))
+            if s >= 1:
                 e_copy(s - 1)
-            if s == n_units + 2:
-                rinv_copy(last)
             run(y_out, *[gi for gi in due if y_on_scalar(gi)])
-            if s == n_units:
-                row_sums(last)
-                recip(last)
-            run(recip, paired(s, 10), one[6])
+            run(recip, paired(s, 10), single(s, 6))
             run(rinv_through_out, paired(s, 10))
-            if s == 10:
-                q_loads((3, 4, 5, 6, 7, 1))
-            run(norm, paired(s, 21), paired(s, 25, 1), single(s, 8))
+            if s in (10, 18, 26):
+                q_loads({10: (3, 4), 18: (1, 5), 26: (6, 7)}[s])
+            run(norm, paired(s, 17), paired(s, 21, 1), single(s, 8))
             maxed = []
             while next_max < n_units and next_max <= s + (3 if passes(unit(next_max)[0]) == 1 else 2):
                 maxs(next_max, 0)
@@ -422,24 +403,44 @@ def tile_mha_t_kernel(tc, q, k, v, W_proj, out):
             run(y_out, *[gi for gi in due if not y_on_scalar(gi)])
             if q_due:
                 qt_copy(q_next)
-            run(o_quant, paired(s, 26), single(s, 10))
-            if s % 2 == 0 and 0 <= s - 4 < n_units - 2:
+            run(o_quant, paired(s, 22), single(s, 10))
+            if s % 2 == 0 and s >= 4:
                 e_quant((s - 4) // 4, (s - 4) % 4, (s - 4) % 4 + 2)
-            if s == n_units + 1:
-                e_quant(last, 2, 3)
-            if s == n_units + 2:
-                e_quant(last, 3, 4)
             if s == 11:
                 v_quant(0)
             if s == 20:
                 v_quant(1)
-            if s == 26:
+            if s == 22:
                 nc.vector.quantize_mx(out=wcod[:].bitcast(FP8X4), scales=wsca[:], in_=wg[:].rearrange("p o h -> p (o h)"))
             maxs(s + 2, 1)
-            run(row_sums, paired(s, 9), one[5])
+            run(row_sums, paired(s, 9), single(s, 5))
             for u in maxed:
                 neg_max(u)
             if 6 <= s < 10:
                 v_regroup(0, s - 6)
             if 14 <= s < 18:
                 v_regroup(1, s - 14)
+
+        pair_a, pair_b = N_PAIRED - 2, N_PAIRED - 1
+        e_quant(last, 0, 2)
+        norm(last - 1)
+        proj(last - 2)
+        e_transposes(n_units - 1)
+        e_copy(n_units - 1)
+        row_sums(last)
+        recip(last)
+        rinv_matmul(last)
+        rinv_copy(last)
+        e_quant(last, 2, 3)
+        e_quant(last, 3, 4)
+        av(last)
+        o_quant(last - 1)
+        y_out(last - 2)
+        norm(last)
+        proj(pair_b)
+        y_out(pair_b)
+        o_quant(last)
+        proj(last - 1)
+        proj(last)
+        y_out(last - 1)
+        y_out(last)

import math
from contextlib import ExitStack

import concourse.mybir as mybir
from concourse.masks import make_identity

S, T, H, D = 4096, 1024, 4, 128
E = H * D
FLOPS = 2 * S * T * D * H + 2 * (512 * 512 + 3584 * 1024) * D * H + 2 * S * E * E

BF16 = mybir.dt.bfloat16
F32 = mybir.dt.float32
U32 = mybir.dt.uint32
U8 = mybir.dt.uint8
FP8X4 = mybir.dt.float8_e4m3fn_x4
ALU = mybir.AluOpType
ACTF = mybir.ActivationFunctionType
AX = mybir.AxisListType

P = 128
SCALE = 1.0 / math.sqrt(D)
MASK_FILL = -131072.0
GROUP_ORDER = list(range(0, 4)) + list(range(8, 20)) + list(range(7, 3, -1)) + list(range(20, 32))
N_PAIRED = 28


def tile_mha_t_kernel(tc, q, k, v, W_proj, out):
    nc = tc.nc
    with ExitStack() as ctx:
        const = ctx.enter_context(tc.tile_pool(name="const", bufs=1))
        work = ctx.enter_context(tc.tile_pool(name="work", bufs=4))
        small = ctx.enter_context(tc.tile_pool(name="small", bufs=6))
        psum = ctx.enter_context(tc.psum_pool(name="psum", bufs=8))

        k_sb = const.tile([P, 2, 4, E], BF16, name="k_sb")
        v_sb = const.tile([P, 2, 4, E], BF16, name="v_sb")
        w_sb = const.tile([P, 4, E], BF16, name="w_sb")
        q_sb = const.tile([P, 32, E], BF16, name="q_sb")
        q_view = q.rearrange("(i p) h d -> p i (h d)", p=P)
        k_view = k.rearrange("(g a c u e) h d -> g e u c a (h d)", g=2, a=2, u=2, e=2)
        for c in range(2):
            cols = slice(c * 2 * D, (c + 1) * 2 * D)
            for u in range(2):
                for e in range(2):
                    nc.sync.dma_start(out=k_sb[e:P:2, 0, 2 * u:2 * u + 2, cols], in_=k_view[0, e, u, :, :, cols])
            if c == 0:
                nc.sync.dma_start(out=q_sb[:, 0:1, :], in_=q_view[:, 0:1, :])
                nc.sync.dma_start(out=q_sb[:, 1:2, :], in_=q_view[:, 1:2, :])
        nc.sync.dma_start(out=q_sb[:, 2:4, :], in_=q_view[:, 2:4, :])
        v_view = v.rearrange("(g c t) h d -> c g t (h d)", g=2, t=4)
        nc.sync.dma_start(out=v_sb[:, 0], in_=v_view[:, 0])
        for u in range(2):
            for e in range(2):
                nc.sync.dma_start(out=k_sb[e:P:2, 1, 2 * u:2 * u + 2, :], in_=k_view[1, e, u])
        nc.sync.dma_start(out=q_sb[:, 8:12, :], in_=q_view[:, 8:12, :])
        nc.sync.dma_start(out=w_sb[:], in_=W_proj.rearrange("(a p) f -> p a f", p=P))
        nc.sync.dma_start(out=v_sb[:, 1], in_=v_view[:, 1])

        def q_loads(blocks):
            for a in blocks:
                nc.sync.dma_start(out=q_sb[:, 4 * a:4 * a + 4, :], in_=q_view[:, 4 * a:4 * a + 4, :])

        ident = const.tile([P, P], BF16, name="ident")
        make_identity(nc, ident[:])
        ident_w = const.tile([P, P], F32, name="ident_w")
        make_identity(nc, ident_w[:])
        maskb = const.tile([P, 2, 32, 2], BF16, name="maskb")
        nc.gpsimd.memset(maskb[:], 0.0)
        for e in range(2):
            nc.gpsimd.affine_select(
                out=maskb[:, :, :, e], in_=maskb[:, :, :, e], pattern=[[-2, 2], [-4, 32]],
                compare_op=ALU.is_ge, fill=MASK_FILL, base=-e, channel_multiplier=1)

        kT = const.tile([P, 2, H, 512], BF16, name="kT")
        vg = const.tile([P, 2, E, 4], BF16, name="vg", align_bytes=64)
        vcod = const.tile([P, 2, E], U32, name="vcod", align_bytes=64)
        vsca = const.tile([P, 2, E], U8, name="vsca", align_bytes=64)
        wg = const.tile([P, E, H], BF16, name="wg", align_bytes=64)
        wcod = const.tile([P, E], U32, name="wcod", align_bytes=64)
        wsca = const.tile([P, E], U8, name="wsca", align_bytes=64)
        warm = const.tile([P, 1], F32, name="warm")
        nc.vector.memset(warm[:], 0.0)
        warm_out = const.tile([P, 1], F32, name="warm_out")
        e_light = []
        for j in range(4):
            e_tile = const.tile([P, 512], BF16, name="e_light%d" % j)
            nc.gpsimd.memset(e_tile[:], 0.0)
            e_light.append(e_tile)

        ctx.enter_context(tc.manual_schedule())
        nc.scalar.activation(out=warm_out[:], in_=warm[:], func=ACTF.Exp)

        n_groups = len(GROUP_ORDER)
        n_units = 4 * n_groups
        st = {}

        def kt_transposes(g, h):
            pk = psum.tile([P, 512], BF16, name="pk", tag="x")
            for t in range(4):
                nc.tensor.transpose(pk[:, t * P:(t + 1) * P], k_sb[:, g, t, h * D:(h + 1) * D], ident[:])
            if (g, h) in ((0, 0), (0, 1), (1, 2), (1, 3)):
                nc.vector.tensor_copy(out=kT[:, g, h, :], in_=pk[:])
            else:
                nc.scalar.copy(out=kT[:, g, h, :], in_=pk[:])

        def passes(i):
            return 1 if i < 4 else 2

        def live_cols(i, g):
            if i < 8 and g == i // 4:
                return 32 * (i % 4 + 1)
            return P

        def live(ap, i, g):
            return ap.rearrange("p (u w) -> p u w", u=2)[:, :, 0:2 * live_cols(i, g)]

        def unit(u):
            return GROUP_ORDER[u // 4], u % 4

        def q_tiles(gj):
            return (gj,) if gj < 2 else (gj, gj + 1)

        def qt_transposes(gj):
            tiles = q_tiles(gj)
            pq = psum.tile([P, len(tiles), E], BF16, name="pq", tag="x")
            for b, g in enumerate(tiles):
                for h in range(H):
                    nc.tensor.transpose(pq[:, b, h * P:(h + 1) * P], q_sb[:, GROUP_ORDER[g], h * D:(h + 1) * D], ident[:])
            st[("pq", gj)] = pq

        def qt_copy(gj):
            tiles = q_tiles(gj)
            qT = work.tile([P, len(tiles), E], BF16, name="qT", tag="qT")
            nc.vector.tensor_copy(out=qT[:], in_=st[("pq", gj)][:])
            for b, g in enumerate(tiles):
                st[("qT", g)] = qT[:, b, :]

        def scores(u, gs):
            if not 0 <= u < n_units:
                return
            i, h = unit(u)
            qT = st[("qT", u // 4)]
            banks = st.setdefault(("s", u), {})
            for g in gs:
                if g >= passes(i):
                    continue
                sg = psum.tile([P, 512], F32, name="sg", tag="x")
                masked = (i < 8) and (g == i // 4)
                nc.tensor.matmul(live(sg[:], i, g), lhsT=qT[:, h * P:(h + 1) * P], rhs=live(kT[:, g, h, :], i, g),
                                 start=True, stop=not masked)
                if masked:
                    j = i % 4
                    nc.tensor.matmul(sg[:].rearrange("p (u w) -> p u w", u=2)[:, :, 64 * j:64 * j + 64], lhsT=ident[:],
                                     rhs=maskb[:].rearrange("p u c e -> p u (c e)"), start=False, stop=True)
                banks[g] = sg

        def maxs(u, g):
            if not 0 <= u < n_units or g >= passes(unit(u)[0]):
                return
            i, h = unit(u)
            if g == 0:
                st[("mx", u)] = small.tile([P, 2], F32, name="mx", tag="mx")
            mx = st[("mx", u)]
            nc.vector.tensor_reduce(out=mx[:, g:g + 1], in_=live(st[("s", u)][g][:], i, g), axis=AX.XY, op=ALU.max)

        def neg_max(u):
            if not 0 <= u < n_units:
                return
            i, h = unit(u)
            mx = st[("mx", u)]
            nb = small.tile([P, 1], F32, name="nb", tag="nb")
            if passes(i) == 2:
                nc.gpsimd.tensor_scalar(out=nb[:], in0=mx[:, 0:1], scalar1=mx[:, 1:2], scalar2=-SCALE,
                                        op0=ALU.max, op1=ALU.mult)
            else:
                nc.gpsimd.tensor_scalar(out=nb[:], in0=mx[:, 0:1], scalar1=-SCALE, scalar2=0.0,
                                        op0=ALU.mult, op1=ALU.add)
            st[("nb", u)] = nb

        def in_group(gi):
            return 2 if gi < N_PAIRED else 1

        def exps(u):
            i, h = unit(u)
            gi = u // 4
            n_in = in_group(gi)
            if h == 0 and gi % n_in == 0:
                st[("rs", gi)] = small.tile([P, n_in * H, 2], F32, name="rs", tag="rs")
            rs = st[("rs", gi - gi % n_in)]
            col = gi % n_in * H + h
            e = e_light[u % 4] if i < 4 else work.tile([P, T], BF16, name="e", tag="e")
            for g in range(passes(i)):
                eg = e[:, g * 512:(g + 1) * 512]
                n_live = live_cols(i, g)
                if n_live < P and i >= 4:
                    nc.gpsimd.memset(eg.rearrange("p (u w) -> p u w", u=2)[:, :, 2 * n_live:2 * P], 0.0)
                nc.scalar.activation(out=live(eg, i, g), in_=live(st[("s", u)][g][:], i, g), func=ACTF.Exp,
                                     bias=st[("nb", u)][:], scale=SCALE, accum_out=rs[:, col, g:g + 1])
            st[("e", u)] = e

        def e_transposes(u):
            i, h = unit(u)
            words = st[("e", u)][:].bitcast(F32)
            pt = psum.tile([P, 4 * P], F32, name="pt", tag="x")
            for j in range(2 * passes(i)):
                nc.tensor.transpose(pt[:, j * P:(j + 1) * P], words[:, j * P:(j + 1) * P], ident_w[:])
            st[("pt", u)] = pt

        def e_copy(u):
            i, h = unit(u)
            np_ = passes(i)
            if h == 0:
                st[("gr", u // 4)] = work.tile([P, H, np_, P, 2], F32, name="gr", tag="gr", bufs=3, align_bytes=64)
            gr = st[("gr", u // 4)]
            src = st[("pt", u)][:, 0:np_ * 256].rearrange("p (g u q) -> p g q u", g=np_, u=2)
            nc.scalar.copy(out=gr[:, h], in_=src)

        def e_quant(gi, h0, h1):
            np_ = passes(GROUP_ORDER[gi])
            if h0 == 0:
                st[("cod", gi)] = work.tile([P, H, np_, P], U32, name="cod", tag="cod", bufs=6, align_bytes=64)
                st[("sca", gi)] = work.tile([P, H, np_, P], U8, name="sca", tag="sca", bufs=6, align_bytes=64)
            nc.vector.quantize_mx(
                out=st[("cod", gi)][:, h0:h1].rearrange("p h g q -> p (h g q)").bitcast(FP8X4),
                scales=st[("sca", gi)][:, h0:h1].rearrange("p h g q -> p (h g q)"),
                in_=st[("gr", gi)][:, h0:h1].rearrange("p h g q u -> p (h g q u)").bitcast(BF16))

        def av(gi, h0=0, h1=H):
            np_ = passes(GROUP_ORDER[gi])
            cod = st[("cod", gi)]
            sca = st[("sca", gi)]
            if h0 == 0:
                o_bank = psum.tile([P, H, P], F32, name="o", tag="x")
                st[("o", gi)] = o_bank
            o = st[("o", gi)]
            for h in range(h0, h1):
                for g in range(np_):
                    nc.tensor.matmul_mx(
                        out=o[:, h, :],
                        lhsT=vcod[:, g, h * D:(h + 1) * D].bitcast(FP8X4), lhsT_scale=vsca[:, g, h * D:(h + 1) * D],
                        rhs=cod[:, h, g, :].bitcast(FP8X4), rhs_scale=sca[:, h, g, :],
                        start=(g == 0), stop=(g == np_ - 1))

        def row_sums(gi):
            rs = st[("rs", gi)]
            if passes(GROUP_ORDER[gi]) == 2:
                rsum = small.tile([P, in_group(gi) * H], F32, name="rsum", tag="rsum")
                nc.gpsimd.tensor_tensor(out=rsum[:], in0=rs[:, :, 0], in1=rs[:, :, 1], op=ALU.add)
                st[("rsum", gi)] = rsum[:]
            else:
                st[("rsum", gi)] = rs[:, :, 0]

        def recip(gi):
            rinv = small.tile([P, in_group(gi) * H], F32, name="rinv", tag="rinv")
            nc.vector.reciprocal(out=rinv[:], in_=st[("rsum", gi)])
            st[("rinv", gi)] = rinv

        def rinv_through_out(gi):
            i = GROUP_ORDER[gi]
            rows = out[i * P:i * P + 2, :].rearrange("a b -> (a b)")
            nc.sync.dma_start(out=rows.rearrange("(q c) -> q c", c=2 * H), in_=st[("rinv", gi)][:])
            rb = work.tile([P, P, 2, H], F32, name="rb", tag="rb", bufs=3)
            nc.sync.dma_start(out=rb[:].rearrange("p q b h -> p (q b h)"), in_=rows.partition_broadcast(P))
            for b in range(2):
                st[("rb", gi + b)] = rb[:, :, b, :]

        def rinv_matmul(gi):
            pr = psum.tile([P, H, P], F32, name="pr", tag="x")
            for h in range(H):
                nc.tensor.transpose(pr[:, h, :], st[("rinv", gi)][:, h:h + 1].to_broadcast([P, P]), ident_w[:])
            st[("pr", gi)] = pr

        def rinv_copy(gi):
            rb = work.tile([P, H, P], F32, name="rb1", tag="rb1", bufs=2)
            nc.scalar.copy(out=rb[:], in_=st[("pr", gi)][:])
            st[("rb", gi)] = rb[:].rearrange("p h q -> p q h")

        def norm(gi):
            n_in = in_group(gi)
            if gi % n_in == 0:
                st[("og", gi)] = work.tile([P, n_in, P, H], BF16, name="og", tag="og", align_bytes=64)
            og = st[("og", gi - gi % n_in)]
            nc.vector.tensor_tensor(out=og[:, gi % n_in], in0=st[("o", gi)][:].rearrange("p h q -> p q h"),
                                    in1=st[("rb", gi)], op=ALU.mult)

        def o_quant(gi):
            n_in = in_group(gi)
            ocod = work.tile([P, n_in, P], U32, name="ocod", tag="ocod", align_bytes=64)
            osca = work.tile([P, n_in, P], U8, name="osca", tag="osca", align_bytes=64)
            nc.vector.quantize_mx(out=ocod[:].rearrange("p b q -> p (b q)").bitcast(FP8X4),
                                  scales=osca[:].rearrange("p b q -> p (b q)"),
                                  in_=st[("og", gi)][:].rearrange("p b q h -> p (b q h)"))
            for b in range(n_in):
                st[("ocod", gi + b)] = ocod[:, b, :]
                st[("osca", gi + b)] = osca[:, b, :]

        def proj(gi):
            parts = 2 if gi == n_groups - 1 else 1
            n = E // parts
            st[("y", gi)] = []
            for b in range(parts):
                y = psum.tile([P, E], F32, name="y", tag="x")
                nc.tensor.matmul_mx(out=y[:, 0:n], lhsT=st[("ocod", gi)].bitcast(FP8X4), lhsT_scale=st[("osca", gi)],
                                    rhs=wcod[:, b * n:(b + 1) * n].bitcast(FP8X4), rhs_scale=wsca[:, b * n:(b + 1) * n],
                                    start=True, stop=True)
                st[("y", gi)].append(y)

        def y_on_scalar(gi):
            return gi % 4 == 3 if gi < N_PAIRED - 2 else gi in (27, 29)

        def y_out(gi):
            i = GROUP_ORDER[gi]
            n = E // len(st[("y", gi)])
            for b, y in enumerate(st[("y", gi)]):
                ysb = work.tile([P, n], F32, name="ysb", tag="ysb", bufs=16)
                if y_on_scalar(gi) or b == 1:
                    nc.scalar.copy(out=ysb[:], in_=y[:, 0:n])
                else:
                    nc.vector.tensor_copy(out=ysb[:], in_=y[:, 0:n])
                queue = nc.scalar if b == 1 else nc.sync
                queue.dma_start(out=out[i * P:(i + 1) * P, b * n:(b + 1) * n], in_=ysb[:])

        def w_transposes(half):
            pw = psum.tile([P, 2, H, P], BF16, name="pw", tag="x")
            for b in range(2):
                for h in range(H):
                    nc.tensor.transpose(pw[:, b, h, :], w_sb[:, 2 * half + b, h * P:(h + 1) * P], ident[:])
            nc.scalar.copy(out=wg[:, half * 2 * P:(half + 1) * 2 * P, :].rearrange("p (b o) h -> p b o h", b=2),
                           in_=pw[:].rearrange("p b h o -> p b o h"))

        def v_regroup(g, piece):
            f0 = 128 * piece
            nc.gpsimd.tensor_scalar(out=vg[:, g, f0:f0 + 128, :], in0=v_sb[:, g, :, f0:f0 + 128].rearrange("p t f -> p f t"),
                                    scalar1=1.0, scalar2=0.0, op0=ALU.mult, op1=ALU.add)

        def v_quant(g):
            nc.vector.quantize_mx(out=vcod[:, g, :].bitcast(FP8X4), scales=vsca[:, g, :],
                                  in_=vg[:, g].rearrange("p f t -> p (f t)"))

        kt_transposes(0, 0)
        qt_transposes(0)
        qt_copy(0)
        kt_transposes(0, 1)
        kt_transposes(0, 2)

        def single(s, offset):
            gi = (s - offset) // 4
            return gi if (s - offset) % 4 == 0 and N_PAIRED <= gi < n_groups else None

        def paired(s, offset, b=0):
            gi = (s - offset) // 4
            return gi + b if (s - offset) % 8 == 0 and 0 <= gi < N_PAIRED else None

        def run(fn, *tiles):
            for gi in tiles:
                if gi is not None:
                    fn(gi)

        last = n_groups - 1

        def results_due(s):
            return [gi for gi in (paired(s, 23), paired(s, 27, 1), single(s, 14)) if gi is not None]

        next_scores = 0
        next_max = 0
        for s in range(-3, n_units):
            run(rinv_matmul, single(s, 7))
            run(rinv_copy, single(s, 7))
            if s >= 0:
                exps(s)
            if s == -2:
                kt_transposes(0, 3)
            if 13 <= s < 17:
                kt_transposes(1, s - 13)
            due = results_due(s)
            while next_scores < n_units and next_scores <= s + (3 if passes(unit(next_scores)[0]) == 1 else 2):
                scores(next_scores, (0,))
                next_scores += 1
            q_next = (s + 6) // 4
            q_due = (s + 6) % 4 == 0 and (q_next == 1 or (1 < q_next < n_groups and q_next % 2 == 0))
            if q_due:
                qt_transposes(q_next)
            if s in (17, 19):
                w_transposes((17, 19).index(s))
            run(proj, *due)
            if s >= 1:
                e_transposes(s - 1)
            scores(s + 2, (1,))
            run(av, paired(s, 16), paired(s, 20, 1), single(s, 7))
            if s >= 1:
                e_copy(s - 1)
            run(y_out, *[gi for gi in due if y_on_scalar(gi)])
            run(recip, paired(s, 10), single(s, 6))
            run(rinv_through_out, paired(s, 10))
            if s in (10, 18, 26):
                q_loads({10: (3, 4), 18: (1, 5), 26: (6, 7)}[s])
            run(norm, paired(s, 17), paired(s, 21, 1), single(s, 8))
            maxed = []
            while next_max < n_units and next_max <= s + (3 if passes(unit(next_max)[0]) == 1 else 2):
                maxs(next_max, 0)
                maxed.append(next_max)
                next_max += 1
            run(y_out, *[gi for gi in due if not y_on_scalar(gi)])
            if q_due:
                qt_copy(q_next)
            run(o_quant, paired(s, 22), single(s, 10))
            if s % 2 == 0 and s >= 4:
                e_quant((s - 4) // 4, (s - 4) % 4, (s - 4) % 4 + 2)
            if s == 11:
                v_quant(0)
            if s == 20:
                v_quant(1)
            if s == 22:
                nc.vector.quantize_mx(out=wcod[:].bitcast(FP8X4), scales=wsca[:], in_=wg[:].rearrange("p o h -> p (o h)"))
            maxs(s + 2, 1)
            run(row_sums, paired(s, 9), single(s, 5))
            for u in maxed:
                neg_max(u)
            if 6 <= s < 10:
                v_regroup(0, s - 6)
            if 14 <= s < 18:
                v_regroup(1, s - 14)

        pair_a, pair_b = N_PAIRED - 2, N_PAIRED - 1
        e_quant(last, 0, 2)
        norm(last - 1)
        proj(last - 2)
        e_transposes(n_units - 1)
        e_copy(n_units - 1)
        row_sums(last)
        recip(last)
        rinv_matmul(last)
        rinv_copy(last)
        e_quant(last, 2, 3)
        e_quant(last, 3, 4)
        av(last)
        o_quant(last - 1)
        y_out(last - 2)
        norm(last)
        proj(pair_b)
        y_out(pair_b)
        o_quant(last)
        proj(last - 1)
        proj(last)
        y_out(last - 1)
        y_out(last)
